import numpy as np
import ml_dtypes


def mxq(x, axis, fmt="e4m3"):
    dtype, down = {"e4m3": (ml_dtypes.float8_e4m3fn, 7), "e5m2": (ml_dtypes.float8_e5m2, 14)}[fmt]
    v = np.moveaxis(np.asarray(x, np.float32).astype(ml_dtypes.bfloat16).astype(np.float64), axis, -1)
    blocks = v.reshape(v.shape[:-1] + (-1, 32))
    amax = np.abs(blocks).max(-1, keepdims=True)
    byte = np.maximum(np.where(amax > 0, np.frexp(amax)[1] - 1 + 127, 0) - down, 1)
    scale = np.exp2(byte - 127.0)
    codes = (blocks / scale).astype(np.float32).astype(dtype).astype(np.float64)
    return np.moveaxis((codes * scale).reshape(v.shape), -1, axis)


WIDE = False


def mx_kscale(k):
    if not WIDE:
        return np.ones(k)
    levels = np.array([10, -10, 5, -5, 0])
    if k % 512:
        return np.exp2(np.random.permutation(np.resize(levels, k // 32))).repeat(32)
    a = np.empty((k // 512, 16))
    for p in range(k // 512):
        a[p, :8] = np.random.permutation(np.resize(levels, 8))
        for g in range(8):
            far = levels[np.abs(levels - a[p, g]) >= 10]
            a[p, g + 8] = far[np.random.randint(len(far))]
    return np.exp2(a.ravel()).repeat(32)


BF16 = ml_dtypes.bfloat16


def bf(x):
    return np.asarray(x, np.float32).astype(BF16)


def f64(x):
    return np.asarray(x).astype(np.float64)


B, E, P, H, HK, D = 4, 128, 384, 4, 2, 128
G = H // HK
S = P + E
SCALING = 1.0 / np.sqrt(D)


def setup_inputs():
    s = mx_kscale(S)
    a = np.log2(s)
    g = s.max() / s
    q = np.random.standard_normal((B, E, H, D)) * 2.0
    k = np.random.standard_normal((B, E, HK, D))
    v = np.random.standard_normal((B, E, HK, D)) * 2.0
    k_cache = np.random.standard_normal((B, P, HK, D))
    v_cache = np.random.standard_normal((B, P, HK, D)) * 2.0
    q[..., 0] = np.log(2.0) * np.sqrt(D)
    k_cache[..., 0] += a[:P][None, :, None]
    k[..., 0] += a[P:][None, :, None]
    v_cache *= g[:P][None, :, None, None]
    v *= g[P:][None, :, None, None]
    return {"q": bf(q), "k": bf(k), "v": bf(v), "k_cache": bf(k_cache), "v_cache": bf(v_cache)}


def reference(q, k, v, k_cache, v_cache):
    k_all = np.concatenate([f64(k_cache), f64(k)], axis=1)
    v_all = np.concatenate([f64(v_cache), f64(v)], axis=1)
    qg = f64(q).reshape(B, E, HK, G, D).transpose(0, 2, 3, 1, 4).reshape(B, HK, G * E, D)
    scores = ((qg @ k_all.transpose(0, 2, 3, 1)) * SCALING).reshape(B, HK, G, E, S)
    visible = np.arange(S)[None, :] <= (P + np.arange(E))[:, None]
    scores = np.where(visible[None, None, None, :, :], scores, -1e30)
    e = np.exp(scores - scores.max(-1, keepdims=True))
    o = mxq(e, 4, "e4m3").reshape(B, HK, G * E, S) @ mxq(v_all, 1, "e4m3").transpose(0, 2, 1, 3)
    o = o.reshape(B, HK, G, E, D) / e.sum(-1, keepdims=True)
    return o.transpose(0, 3, 1, 2, 4).reshape(B * E, H * D)

@@ -1,0 +1,321 @@
+import math
+from contextlib import ExitStack
+
+import concourse.mybir as mybir
+from concourse.masks import make_identity
+
+BF16 = mybir.dt.bfloat16
+F32 = mybir.dt.float32
+U32 = mybir.dt.uint32
+U8 = mybir.dt.uint8
+FP8X4 = mybir.dt.float8_e4m3fn_x4
+ALU = mybir.AluOpType
+ACT = mybir.ActivationFunctionType
+AX = mybir.AxisListType
+
+B = 4
+E = 128
+PREFIX = 384
+S = PREFIX + E
+H = 4
+HK = 2
+G = H // HK
+D = 128
+P = 128
+SCALING = 1.0 / math.sqrt(D)
+HIDDEN = -1.0e30
+
+FLOPS = 2 * 2 * B * H * E * S * D
+
+
+N_HEADS = B * H
+N_PAIRS = B * HK
+
+
+def sequence_that_starts_at(n):
+    return n // H if 0 <= n < N_HEADS and n % H == 0 else None
+
+
+def pair_that_ends_at(n):
+    return n // G if 0 <= n < N_HEADS and n % G == G - 1 else None
+
+
+def tile_radixattention_s_kernel(tc, q, k, v, k_cache, v_cache, out):
+    nc = tc.nc
+    with ExitStack() as ctx:
+        consts = ctx.enter_context(tc.tile_pool(name="consts", bufs=1))
+        keep = ctx.enter_context(tc.tile_pool(name="keep", bufs=1))
+        banks = ctx.enter_context(tc.psum_pool(name="banks", bufs=8))
+        ctx.enter_context(tc.manual_schedule())
+
+        ident_bf = consts.tile([P, P], BF16, name="ident_bf")
+        make_identity(nc, ident_bf[:])
+        causal = consts.tile([P, E], F32, name="causal")
+        nc.gpsimd.memset(causal[:], 0.0)
+        nc.gpsimd.affine_select(
+            out=causal[:],
+            in_=causal[:],
+            compare_op=ALU.is_ge,
+            fill=HIDDEN,
+            base=0,
+            pattern=[[-1, E]],
+            channel_multiplier=1,
+        )
+        ident_f32 = consts.tile([P, P], F32, name="ident_f32")
+        make_identity(nc, ident_f32[:])
+        warm_in = consts.tile([P, 1], F32, name="warm_in")
+        warm_out = consts.tile([P, 1], F32, name="warm_out")
+        nc.vector.memset(warm_in[:], 0.0)
+        nc.scalar.activation(out=warm_out[:], in_=warm_in[:], func=ACT.Exp)
+
+        q_rows, k_rows, v_rows = {}, {}, {}
+        qT_ps, kT_ps, qT, kT = {}, {}, {}, {}
+        v_grouped, v_codes, v_scales = {}, {}, {}
+        diag_ps, masked, diag_max, prefix_max, neg_max = {}, {}, {}, {}, {}
+        prefix_sum, diag_sum, row_sum, inv_sum = {}, {}, {}, {}
+        prefix_ps, e_rows = {}, {}
+        eT_ps, e_grouped, e_codes, e_scales, o_ps = {}, {}, {}, {}, {}
+
+        def load_qk(b):
+            q_rows[b] = keep.tile([P, H * D], BF16, name="q_rows%d" % b)
+            nc.sync.dma_start(out=q_rows[b][:], in_=q[b].rearrange("e h d -> e (h d)"))
+            k_rows[b] = keep.tile([P, S // P, HK * D], BF16, name="k_rows%d" % b)
+            nc.sync.dma_start(
+                out=k_rows[b][:, 0 : PREFIX // P, :],
+                in_=k_cache[b].rearrange("(t p) g d -> p t (g d)", p=P),
+            )
+            nc.sync.dma_start(
+                out=k_rows[b][:, PREFIX // P, :], in_=k[b].rearrange("e g d -> e (g d)")
+            )
+
+        def load_v(b):
+            v_rows[b] = keep.tile([P, 4, HK * D], BF16, name="v_rows%d" % b)
+            nc.sync.dma_start(
+                out=v_rows[b][0 : PREFIX // 4].rearrange("p t c -> p (t c)"),
+                in_=v_cache[b].rearrange("(p t) g d -> p (t g d)", t=4),
+            )
+            nc.sync.dma_start(
+                out=v_rows[b][PREFIX // 4 : P].rearrange("p t c -> p (t c)"),
+                in_=v[b].rearrange("(p t) g d -> p (t g d)", t=4),
+            )
+
+        def transpose_qk(b):
+            qT_ps[b] = banks.tile([P, H * E], BF16, name="qT_ps", tag="bank")
+            for h in range(H):
+                cols = slice(h * D, (h + 1) * D)
+                nc.tensor.transpose(qT_ps[b][:, cols], q_rows[b][:, cols], ident_bf[:])
+            for g in range(HK):
+                kT_ps[b, g] = banks.tile([P, S], BF16, name="kT_ps", tag="bank")
+                for t in range(S // P):
+                    nc.tensor.transpose(
+                        kT_ps[b, g][:, t * P : (t + 1) * P],
+                        k_rows[b][:, t, g * D : (g + 1) * D],
+                        ident_bf[:],
+                    )
+
+        def copy_qk(b):
+            qT[b] = keep.tile([P, H * E], BF16, name="qT%d" % b)
+            kT[b] = keep.tile([P, HK, S], BF16, name="kT%d" % b)
+            nc.scalar.copy(out=qT[b][:], in_=qT_ps[b][:])
+            for g in range(HK):
+                nc.scalar.copy(out=kT[b][:, g, :], in_=kT_ps[b, g][:])
+
+        def regroup_v(b):
+            v_grouped[b] = keep.tile(
+                [P, HK * D, 4], BF16, name="v_grouped%d" % b, align_bytes=64
+            )
+            nc.gpsimd.tensor_scalar(
+                out=v_grouped[b][:],
+                in0=v_rows[b][:].rearrange("p t c -> p c t"),
+                scalar1=1.0,
+                scalar2=0.0,
+                op0=ALU.mult,
+                op1=ALU.add,
+            )
+
+        def quantise_v(b):
+            v_codes[b] = keep.tile([P, HK * D], U32, name="v_codes%d" % b, align_bytes=64)
+            v_scales[b] = keep.tile([P, HK * D], U8, name="v_scales%d" % b, align_bytes=64)
+            nc.vector.quantize_mx(
+                out=v_codes[b][:].bitcast(FP8X4),
+                scales=v_scales[b][:],
+                in_=v_grouped[b][:].rearrange("p c t -> p (c t)"),
+            )
+
+        def score_diag(b):
+            diag_ps[b] = banks.tile([P, H, E], F32, name="diag_ps", tag="bank")
+            prefix_max[b] = keep.tile([P, H], F32, name="prefix_max%d" % b)
+            neg_max[b] = keep.tile([P, H], F32, name="neg_max%d" % b)
+            prefix_sum[b] = keep.tile([P, H], F32, name="prefix_sum%d" % b)
+            diag_sum[b] = keep.tile([P, H], F32, name="diag_sum%d" % b)
+            for h in range(H):
+                nc.tensor.matmul(
+                    out=diag_ps[b][:, h, :],
+                    lhsT=qT[b][:, h * E : (h + 1) * E],
+                    rhs=kT[b][:, h // G, PREFIX:S],
+                    start=True,
+                    stop=True,
+                )
+
+        def mask_diag(b):
+            masked[b] = keep.tile([P, H, E], F32, name="masked%d" % b)
+            nc.vector.tensor_tensor(
+                out=masked[b][:],
+                in0=diag_ps[b][:],
+                in1=causal[:].unsqueeze(1).to_broadcast([P, H, E]),
+                op=ALU.add,
+            )
+
+        def max_diag(b):
+            diag_max[b] = keep.tile([P, H], F32, name="diag_max%d" % b)
+            nc.vector.tensor_reduce(out=diag_max[b][:], in_=masked[b][:], axis=AX.X, op=ALU.max)
+
+        def score_prefix(n):
+            b, h = divmod(n, H)
+            prefix_ps[n] = banks.tile([P, PREFIX], F32, name="prefix_ps", tag="bank")
+            nc.tensor.matmul(
+                out=prefix_ps[n][:],
+                lhsT=qT[b][:, h * E : (h + 1) * E],
+                rhs=kT[b][:, h // G, 0:PREFIX],
+                start=True,
+                stop=True,
+            )
+
+        def max_prefix(n):
+            b, h = divmod(n, H)
+            nc.vector.tensor_reduce(
+                out=prefix_max[b][:, h : h + 1], in_=prefix_ps[n][:], axis=AX.X, op=ALU.max
+            )
+
+        def exp_bias(n):
+            b, h = divmod(n, H)
+            nc.vector.tensor_scalar(
+                out=neg_max[b][:, h : h + 1],
+                in0=prefix_max[b][:, h : h + 1],
+                scalar1=diag_max[b][:, h : h + 1],
+                scalar2=-SCALING,
+                op0=ALU.max,
+                op1=ALU.mult,
+            )
+
+        def exponentials(n):
+            b, h = divmod(n, H)
+            e_rows[n] = keep.tile([P, S], BF16, name="e_rows%d" % n)
+            nc.scalar.activation(
+                out=e_rows[n][:, 0:PREFIX],
+                in_=prefix_ps[n][:],
+                func=ACT.Exp,
+                bias=neg_max[b][:, h : h + 1],
+                scale=SCALING,
+                accum_out=prefix_sum[b][:, h : h + 1],
+            )
+            nc.scalar.activation(
+                out=e_rows[n][:, PREFIX:S],
+                in_=masked[b][:, h, :],
+                func=ACT.Exp,
+                bias=neg_max[b][:, h : h + 1],
+                scale=SCALING,
+                accum_out=diag_sum[b][:, h : h + 1],
+            )
+
+        def transpose_e(n):
+            eT_ps[n] = banks.tile([P, 2, E], F32, name="eT_ps", tag="bank")
+            words = e_rows[n][:].bitcast(F32)
+            for u in range(2):
+                nc.tensor.transpose(eT_ps[n][:, u, :], words[:, u : 2 * P : 2], ident_f32[:])
+
+        def regroup_e(n):
+            p, a = divmod(n, G)
+            if a == 0:
+                e_grouped[p] = keep.tile(
+                    [P, G, E * 4], BF16, name="e_grouped%d" % p, align_bytes=64
+                )
+            nc.scalar.copy(
+                out=e_grouped[p][:, a, :].bitcast(F32).rearrange("p (i u) -> p i u", u=2),
+                in_=eT_ps[n][:].rearrange("p u i -> p i u"),
+            )
+
+        def quantise_e(p):
+            e_codes[p] = keep.tile([P, G * E], U32, name="e_codes%d" % p, align_bytes=64)
+            e_scales[p] = keep.tile([P, G * E], U8, name="e_scales%d" % p, align_bytes=64)
+            nc.vector.quantize_mx(
+                out=e_codes[p][:].bitcast(FP8X4),
+                scales=e_scales[p][:],
+                in_=e_grouped[p][:].rearrange("p a c -> p (a c)"),
+            )
+
+        def multiply_v(p):
+            b, g = divmod(p, HK)
+            if g == 0:
+                o_ps[b] = banks.tile([P, H, D], F32, name="o_ps", tag="bank")
+            for a in range(G):
+                nc.tensor.matmul_mx(
+                    out=o_ps[b][:, g * G + a, :],
+                    lhsT=e_codes[p][:, a * E : (a + 1) * E].bitcast(FP8X4),
+                    lhsT_scale=e_scales[p][:, a * E : (a + 1) * E],
+                    rhs=v_codes[b][:, g * D : (g + 1) * D].bitcast(FP8X4),
+                    rhs_scale=v_scales[b][:, g * D : (g + 1) * D],
+                    start=True,
+                    stop=True,
+                )
+
+        def sum_rows(b):
+            row_sum[b] = keep.tile([P, H], F32, name="row_sum%d" % b)
+            nc.vector.tensor_tensor(
+                out=row_sum[b][:], in0=prefix_sum[b][:], in1=diag_sum[b][:], op=ALU.add
+            )
+
+        def invert_sums(b):
+            inv_sum[b] = keep.tile([P, H], F32, name="inv_sum%d" % b)
+            nc.vector.reciprocal(out=inv_sum[b][:], in_=row_sum[b][:])
+
+        def normalise_and_store(b, g):
+            heads = slice(g * G, (g + 1) * G)
+            o_sb = keep.tile([P, G, D], F32, name="o_sb%d_%d" % (b, g))
+            nc.vector.tensor_tensor(
+                out=o_sb[:],
+                in0=o_ps[b][:, heads, :],
+                in1=inv_sum[b][:, heads].unsqueeze(2).to_broadcast([P, G, D]),
+                op=ALU.mult,
+            )
+            nc.sync.dma_start(
+                out=out[b * E : (b + 1) * E, g * G * D : (g + 1) * G * D],
+                in_=o_sb[:].rearrange("p a d -> p (a d)"),
+            )
+
+        def when(index, stage):
+            if index is not None:
+                stage(index)
+
+        def unit(n):
+            return n if 0 <= n < N_HEADS else None
+
+        for b in range(B):
+            load_qk(b)
+            load_v(b)
+        for b in range(B):
+            regroup_v(b)
+
+        for s in range(-5, N_HEADS + 4):
+            when(sequence_that_starts_at(s + 5), transpose_qk)
+            when(sequence_that_starts_at(s + 4), score_diag)
+            when(unit(s + 3), score_prefix)
+
+            finished = sequence_that_starts_at(s - 7)
+            when(unit(s + 2), max_prefix)
+            when(sequence_that_starts_at(s + 1), quantise_v)
+            when(sequence_that_starts_at(s + 3), mask_diag)
+            when(sequence_that_starts_at(s + 2), max_diag)
+            when(pair_that_ends_at(s - 3), quantise_e)
+            when(sequence_that_starts_at(s - 5), sum_rows)
+            when(sequence_that_starts_at(s - 6), invert_sums)
+            if finished is not None:
+                normalise_and_store(finished, 0)
+                normalise_and_store(finished, 1)
+            when(unit(s + 2), exp_bias)
+
+            when(unit(s), exponentials)
+            when(unit(s), transpose_e)
+            when(pair_that_ends_at(s - 3), multiply_v)
+            when(unit(s - 1), regroup_e)
+            when(sequence_that_starts_at(s + 5), copy_qk)

@@ -50,16 +50,16 @@ def tile_radixattention_s_kernel(tc, q, k, v, k_cache, v_cache, out):
 
         ident_bf = consts.tile([P, P], BF16, name="ident_bf")
         make_identity(nc, ident_bf[:])
-        causal = consts.tile([P, E], F32, name="causal")
-        nc.gpsimd.memset(causal[:], 0.0)
+        hidden_t = consts.tile([P, E], F32, name="hidden_t")
+        nc.gpsimd.memset(hidden_t[:], 0.0)
         nc.gpsimd.affine_select(
-            out=causal[:],
-            in_=causal[:],
+            out=hidden_t[:],
+            in_=hidden_t[:],
             compare_op=ALU.is_ge,
             fill=HIDDEN,
             base=0,
-            pattern=[[-1, E]],
-            channel_multiplier=1,
+            pattern=[[1, E]],
+            channel_multiplier=-1,
         )
         ident_f32 = consts.tile([P, P], F32, name="ident_f32")
         make_identity(nc, ident_f32[:])
@@ -71,9 +71,8 @@ def tile_radixattention_s_kernel(tc, q, k, v, k_cache, v_cache, out):
         q_rows, k_rows, v_rows = {}, {}, {}
         qT_ps, kT_ps, qT, kT = {}, {}, {}, {}
         v_grouped, v_codes, v_scales = {}, {}, {}
-        diag_ps, masked, diag_max, prefix_max, neg_max = {}, {}, {}, {}, {}
-        prefix_sum, diag_sum, row_sum, inv_sum = {}, {}, {}, {}
-        prefix_ps, e_rows = {}, {}
+        row_max, neg_max, row_sum, inv_sum = {}, {}, {}, {}
+        score_ps, e_rows = {}, {}
         eT_ps, e_grouped, e_codes, e_scales, o_ps = {}, {}, {}, {}, {}
 
         def load_qk(b):
@@ -91,11 +90,15 @@ def tile_radixattention_s_kernel(tc, q, k, v, k_cache, v_cache, out):
         def load_v(b):
             v_rows[b] = keep.tile([P, 4, HK * D], BF16, name="v_rows%d" % b)
             nc.sync.dma_start(
-                out=v_rows[b][0 : PREFIX // 4].rearrange("p t c -> p (t c)"),
-                in_=v_cache[b].rearrange("(p t) g d -> p (t g d)", t=4),
+                out=v_rows[b][0:64].rearrange("p t c -> p (t c)"),
+                in_=v_cache[b, 0:256].rearrange("(p t) g d -> p (t g d)", t=4),
             )
             nc.sync.dma_start(
-                out=v_rows[b][PREFIX // 4 : P].rearrange("p t c -> p (t c)"),
+                out=v_rows[b][64:96].rearrange("p t c -> p (t c)"),
+                in_=v_cache[b, 256:PREFIX].rearrange("(p t) g d -> p (t g d)", t=4),
+            )
+            nc.sync.dma_start(
+                out=v_rows[b][96:P].rearrange("p t c -> p (t c)"),
                 in_=v[b].rearrange("(p t) g d -> p (t g d)", t=4),
             )
 
@@ -142,80 +145,55 @@ def tile_radixattention_s_kernel(tc, q, k, v, k_cache, v_cache, out):
                 in_=v_grouped[b][:].rearrange("p c t -> p (c t)"),
             )
 
-        def score_diag(b):
-            diag_ps[b] = banks.tile([P, H, E], F32, name="diag_ps", tag="bank")
-            prefix_max[b] = keep.tile([P, H], F32, name="prefix_max%d" % b)
-            neg_max[b] = keep.tile([P, H], F32, name="neg_max%d" % b)
-            prefix_sum[b] = keep.tile([P, H], F32, name="prefix_sum%d" % b)
-            diag_sum[b] = keep.tile([P, H], F32, name="diag_sum%d" % b)
-            for h in range(H):
-                nc.tensor.matmul(
-                    out=diag_ps[b][:, h, :],
-                    lhsT=qT[b][:, h * E : (h + 1) * E],
-                    rhs=kT[b][:, h // G, PREFIX:S],
-                    start=True,
-                    stop=True,
-                )
-
-        def mask_diag(b):
-            masked[b] = keep.tile([P, H, E], F32, name="masked%d" % b)
-            nc.vector.tensor_tensor(
-                out=masked[b][:],
-                in0=diag_ps[b][:],
-                in1=causal[:].unsqueeze(1).to_broadcast([P, H, E]),
-                op=ALU.add,
-            )
-
-        def max_diag(b):
-            diag_max[b] = keep.tile([P, H], F32, name="diag_max%d" % b)
-            nc.vector.tensor_reduce(out=diag_max[b][:], in_=masked[b][:], axis=AX.X, op=ALU.max)
-
-        def score_prefix(n):
+        def score(n):
             b, h = divmod(n, H)
-            prefix_ps[n] = banks.tile([P, PREFIX], F32, name="prefix_ps", tag="bank")
+            if h == 0:
+                row_max[b] = keep.tile([P, H], F32, name="row_max%d" % b)
+                neg_max[b] = keep.tile([P, H], F32, name="neg_max%d" % b)
+                row_sum[b] = keep.tile([P, H], F32, name="row_sum%d" % b)
+            score_ps[n] = banks.tile([P, S], F32, name="score_ps", tag="bank")
             nc.tensor.matmul(
-                out=prefix_ps[n][:],
+                out=score_ps[n][:],
                 lhsT=qT[b][:, h * E : (h + 1) * E],
-                rhs=kT[b][:, h // G, 0:PREFIX],
+                rhs=kT[b][:, h // G, :],
                 start=True,
+                stop=False,
+            )
+            nc.tensor.matmul(
+                out=score_ps[n][:, PREFIX:S],
+                lhsT=hidden_t[:],
+                rhs=ident_f32[:],
+                is_transpose=True,
+                start=False,
                 stop=True,
             )
 
-        def max_prefix(n):
+        def max_scores(n):
             b, h = divmod(n, H)
             nc.vector.tensor_reduce(
-                out=prefix_max[b][:, h : h + 1], in_=prefix_ps[n][:], axis=AX.X, op=ALU.max
+                out=row_max[b][:, h : h + 1], in_=score_ps[n][:], axis=AX.X, op=ALU.max
             )
 
         def exp_bias(n):
             b, h = divmod(n, H)
             nc.vector.tensor_scalar(
                 out=neg_max[b][:, h : h + 1],
-                in0=prefix_max[b][:, h : h + 1],
-                scalar1=diag_max[b][:, h : h + 1],
-                scalar2=-SCALING,
-                op0=ALU.max,
-                op1=ALU.mult,
+                in0=row_max[b][:, h : h + 1],
+                scalar1=-SCALING,
+                scalar2=None,
+                op0=ALU.mult,
             )
 
         def exponentials(n):
             b, h = divmod(n, H)
             e_rows[n] = keep.tile([P, S], BF16, name="e_rows%d" % n)
             nc.scalar.activation(
-                out=e_rows[n][:, 0:PREFIX],
-                in_=prefix_ps[n][:],
+                out=e_rows[n][:],
+                in_=score_ps[n][:],
                 func=ACT.Exp,
                 bias=neg_max[b][:, h : h + 1],
                 scale=SCALING,
-                accum_out=prefix_sum[b][:, h : h + 1],
-            )
-            nc.scalar.activation(
-                out=e_rows[n][:, PREFIX:S],
-                in_=masked[b][:, h, :],
-                func=ACT.Exp,
-                bias=neg_max[b][:, h : h + 1],
-                scale=SCALING,
-                accum_out=diag_sum[b][:, h : h + 1],
+                accum_out=row_sum[b][:, h : h + 1],
             )
 
         def transpose_e(n):
@@ -259,12 +237,6 @@ def tile_radixattention_s_kernel(tc, q, k, v, k_cache, v_cache, out):
                     stop=True,
                 )
 
-        def sum_rows(b):
-            row_sum[b] = keep.tile([P, H], F32, name="row_sum%d" % b)
-            nc.vector.tensor_tensor(
-                out=row_sum[b][:], in0=prefix_sum[b][:], in1=diag_sum[b][:], op=ALU.add
-            )
-
         def invert_sums(b):
             inv_sum[b] = keep.tile([P, H], F32, name="inv_sum%d" % b)
             nc.vector.reciprocal(out=inv_sum[b][:], in_=row_sum[b][:])
@@ -298,16 +270,12 @@ def tile_radixattention_s_kernel(tc, q, k, v, k_cache, v_cache, out):
 
         for s in range(-5, N_HEADS + 4):
             when(sequence_that_starts_at(s + 5), transpose_qk)
-            when(sequence_that_starts_at(s + 4), score_diag)
-            when(unit(s + 3), score_prefix)
+            when(unit(s + 3), score)
 
             finished = sequence_that_starts_at(s - 7)
-            when(unit(s + 2), max_prefix)
+            when(unit(s + 2), max_scores)
             when(sequence_that_starts_at(s + 1), quantise_v)
-            when(sequence_that_starts_at(s + 3), mask_diag)
-            when(sequence_that_starts_at(s + 2), max_diag)
             when(pair_that_ends_at(s - 3), quantise_e)
-            when(sequence_that_starts_at(s - 5), sum_rows)
             when(sequence_that_starts_at(s - 6), invert_sums)
             if finished is not None:
                 normalise_and_store(finished, 0)

@@ -45,7 +45,7 @@ def tile_radixattention_s_kernel(tc, q, k, v, k_cache, v_cache, out):
     with ExitStack() as ctx:
         consts = ctx.enter_context(tc.tile_pool(name="consts", bufs=1))
         keep = ctx.enter_context(tc.tile_pool(name="keep", bufs=1))
-        banks = ctx.enter_context(tc.psum_pool(name="banks", bufs=8))
+        banks = ctx.enter_context(tc.psum_pool(name="banks", bufs=1))
         ctx.enter_context(tc.manual_schedule())
 
         ident_bf = consts.tile([P, P], BF16, name="ident_bf")
@@ -63,6 +63,11 @@ def tile_radixattention_s_kernel(tc, q, k, v, k_cache, v_cache, out):
         )
         ident_f32 = consts.tile([P, P], F32, name="ident_f32")
         make_identity(nc, ident_f32[:])
+        ident_t = consts.tile([P, P], F32, name="ident_t")
+        nc.vector.tensor_copy(
+            out=ident_t[:].rearrange("p (t r) -> p t r", t=4),
+            in_=ident_f32[:].rearrange("p (r t) -> p t r", t=4),
+        )
         warm_in = consts.tile([P, 1], F32, name="warm_in")
         warm_out = consts.tile([P, 1], F32, name="warm_out")
         nc.vector.memset(warm_in[:], 0.0)
@@ -75,53 +80,49 @@ def tile_radixattention_s_kernel(tc, q, k, v, k_cache, v_cache, out):
         score_ps, e_rows = {}, {}
         eT_ps, e_grouped, e_codes, e_scales, o_ps = {}, {}, {}, {}, {}
 
+        def load_keys(rows, cached, extend):
+            for partitions, source in (
+                (slice(0, 64), cached[0:256]),
+                (slice(64, 96), cached[256:PREFIX]),
+                (slice(96, P), extend),
+            ):
+                nc.sync.dma_start(
+                    out=rows[partitions].rearrange("p t c -> p (t c)"),
+                    in_=source.rearrange("(p t) g d -> p (t g d)", t=4),
+                )
+
         def load_qk(b):
             q_rows[b] = keep.tile([P, H * D], BF16, name="q_rows%d" % b)
             nc.sync.dma_start(out=q_rows[b][:], in_=q[b].rearrange("e h d -> e (h d)"))
-            k_rows[b] = keep.tile([P, S // P, HK * D], BF16, name="k_rows%d" % b)
-            nc.sync.dma_start(
-                out=k_rows[b][:, 0 : PREFIX // P, :],
-                in_=k_cache[b].rearrange("(t p) g d -> p t (g d)", p=P),
-            )
-            nc.sync.dma_start(
-                out=k_rows[b][:, PREFIX // P, :], in_=k[b].rearrange("e g d -> e (g d)")
-            )
+            k_rows[b] = keep.tile([P, 4, HK * D], BF16, name="k_rows%d" % b)
+            load_keys(k_rows[b], k_cache[b], k[b])
 
         def load_v(b):
             v_rows[b] = keep.tile([P, 4, HK * D], BF16, name="v_rows%d" % b)
-            nc.sync.dma_start(
-                out=v_rows[b][0:64].rearrange("p t c -> p (t c)"),
-                in_=v_cache[b, 0:256].rearrange("(p t) g d -> p (t g d)", t=4),
-            )
-            nc.sync.dma_start(
-                out=v_rows[b][64:96].rearrange("p t c -> p (t c)"),
-                in_=v_cache[b, 256:PREFIX].rearrange("(p t) g d -> p (t g d)", t=4),
-            )
-            nc.sync.dma_start(
-                out=v_rows[b][96:P].rearrange("p t c -> p (t c)"),
-                in_=v[b].rearrange("(p t) g d -> p (t g d)", t=4),
-            )
+            load_keys(v_rows[b], v_cache[b], v[b])
 
-        def transpose_qk(b):
-            qT_ps[b] = banks.tile([P, H * E], BF16, name="qT_ps", tag="bank")
+        def transpose_q(b):
+            qT_ps[b] = banks.tile([P, H * E], BF16, name="qT_ps", tag="work", bufs=3)
             for h in range(H):
                 cols = slice(h * D, (h + 1) * D)
                 nc.tensor.transpose(qT_ps[b][:, cols], q_rows[b][:, cols], ident_bf[:])
-            for g in range(HK):
-                kT_ps[b, g] = banks.tile([P, S], BF16, name="kT_ps", tag="bank")
-                for t in range(S // P):
-                    nc.tensor.transpose(
-                        kT_ps[b, g][:, t * P : (t + 1) * P],
-                        k_rows[b][:, t, g * D : (g + 1) * D],
-                        ident_bf[:],
-                    )
 
-        def copy_qk(b):
+        def transpose_k(b, g):
+            kT_ps[b, g] = banks.tile([P, S], BF16, name="kT_ps", tag="work", bufs=3)
+            for t in range(S // P):
+                nc.tensor.transpose(
+                    kT_ps[b, g][:, t * P : (t + 1) * P],
+                    k_rows[b][:, t, g * D : (g + 1) * D],
+                    ident_bf[:],
+                )
+
+        def copy_q(b):
             qT[b] = keep.tile([P, H * E], BF16, name="qT%d" % b)
-            kT[b] = keep.tile([P, HK, S], BF16, name="kT%d" % b)
             nc.scalar.copy(out=qT[b][:], in_=qT_ps[b][:])
-            for g in range(HK):
-                nc.scalar.copy(out=kT[b][:, g, :], in_=kT_ps[b, g][:])
+
+        def copy_k(b, g, copy):
+            kT[b, g] = keep.tile([P, S], BF16, name="kT%d_%d" % (b, g))
+            copy(out=kT[b, g][:], in_=kT_ps[b, g][:])
 
         def regroup_v(b):
             v_grouped[b] = keep.tile(
@@ -151,18 +152,18 @@ def tile_radixattention_s_kernel(tc, q, k, v, k_cache, v_cache, out):
                 row_max[b] = keep.tile([P, H], F32, name="row_max%d" % b)
                 neg_max[b] = keep.tile([P, H], F32, name="neg_max%d" % b)
                 row_sum[b] = keep.tile([P, H], F32, name="row_sum%d" % b)
-            score_ps[n] = banks.tile([P, S], F32, name="score_ps", tag="bank")
+            score_ps[n] = banks.tile([P, S], F32, name="score_ps", tag="score", bufs=3)
             nc.tensor.matmul(
                 out=score_ps[n][:],
                 lhsT=qT[b][:, h * E : (h + 1) * E],
-                rhs=kT[b][:, h // G, :],
+                rhs=kT[b, h // G][:],
                 start=True,
                 stop=False,
             )
             nc.tensor.matmul(
-                out=score_ps[n][:, PREFIX:S],
+                out=score_ps[n][:].rearrange("p (t j) -> p t j", t=4)[:, :, PREFIX // 4 : P],
                 lhsT=hidden_t[:],
-                rhs=ident_f32[:],
+                rhs=ident_t[:],
                 is_transpose=True,
                 start=False,
                 stop=True,
@@ -188,8 +189,8 @@ def tile_radixattention_s_kernel(tc, q, k, v, k_cache, v_cache, out):
             b, h = divmod(n, H)
             e_rows[n] = keep.tile([P, S], BF16, name="e_rows%d" % n)
             nc.scalar.activation(
-                out=e_rows[n][:],
-                in_=score_ps[n][:],
+                out=e_rows[n][:].rearrange("p (u j x) -> p u j x", u=2, x=2),
+                in_=score_ps[n][:].rearrange("p (u x j) -> p u j x", u=2, x=2),
                 func=ACT.Exp,
                 bias=neg_max[b][:, h : h + 1],
                 scale=SCALING,
@@ -197,10 +198,10 @@ def tile_radixattention_s_kernel(tc, q, k, v, k_cache, v_cache, out):
             )
 
         def transpose_e(n):
-            eT_ps[n] = banks.tile([P, 2, E], F32, name="eT_ps", tag="bank")
+            eT_ps[n] = banks.tile([P, 2, E], F32, name="eT_ps", tag="work", bufs=3)
             words = e_rows[n][:].bitcast(F32)
             for u in range(2):
-                nc.tensor.transpose(eT_ps[n][:, u, :], words[:, u : 2 * P : 2], ident_f32[:])
+                nc.tensor.transpose(eT_ps[n][:, u, :], words[:, u * P : (u + 1) * P], ident_f32[:])
 
         def regroup_e(n):
             p, a = divmod(n, G)
@@ -224,11 +225,10 @@ def tile_radixattention_s_kernel(tc, q, k, v, k_cache, v_cache, out):
 
         def multiply_v(p):
             b, g = divmod(p, HK)
-            if g == 0:
-                o_ps[b] = banks.tile([P, H, D], F32, name="o_ps", tag="bank")
+            o_ps[p] = banks.tile([P, G, D], F32, name="o_ps", tag="o", bufs=2)
             for a in range(G):
                 nc.tensor.matmul_mx(
-                    out=o_ps[b][:, g * G + a, :],
+                    out=o_ps[p][:, a, :],
                     lhsT=e_codes[p][:, a * E : (a + 1) * E].bitcast(FP8X4),
                     lhsT_scale=e_scales[p][:, a * E : (a + 1) * E],
                     rhs=v_codes[b][:, g * D : (g + 1) * D].bitcast(FP8X4),
@@ -241,13 +241,13 @@ def tile_radixattention_s_kernel(tc, q, k, v, k_cache, v_cache, out):
             inv_sum[b] = keep.tile([P, H], F32, name="inv_sum%d" % b)
             nc.vector.reciprocal(out=inv_sum[b][:], in_=row_sum[b][:])
 
-        def normalise_and_store(b, g):
-            heads = slice(g * G, (g + 1) * G)
-            o_sb = keep.tile([P, G, D], F32, name="o_sb%d_%d" % (b, g))
+        def normalise_and_store(p):
+            b, g = divmod(p, HK)
+            o_sb = keep.tile([P, G, D], F32, name="o_sb%d" % p)
             nc.vector.tensor_tensor(
                 out=o_sb[:],
-                in0=o_ps[b][:, heads, :],
-                in1=inv_sum[b][:, heads].unsqueeze(2).to_broadcast([P, G, D]),
+                in0=o_ps[p][:],
+                in1=inv_sum[b][:, g * G : (g + 1) * G].unsqueeze(2).to_broadcast([P, G, D]),
                 op=ALU.mult,
             )
             nc.sync.dma_start(
@@ -268,22 +268,23 @@ def tile_radixattention_s_kernel(tc, q, k, v, k_cache, v_cache, out):
         for b in range(B):
             regroup_v(b)
 
-        for s in range(-5, N_HEADS + 4):
-            when(sequence_that_starts_at(s + 5), transpose_qk)
-            when(unit(s + 3), score)
+        for s in range(-5, N_HEADS + 6):
+            when(unit(s + 2), score)
+            when(unit(s - 1), transpose_e)
+            when(pair_that_ends_at(s - 3), multiply_v)
+            when(sequence_that_starts_at(s + 5), transpose_q)
+            when(sequence_that_starts_at(s + 5), lambda b: transpose_k(b, 0))
+            when(sequence_that_starts_at(s + 2 if s < 0 else s + 3), lambda b: transpose_k(b, 1))
 
-            finished = sequence_that_starts_at(s - 7)
-            when(unit(s + 2), max_scores)
-            when(sequence_that_starts_at(s + 1), quantise_v)
-            when(pair_that_ends_at(s - 3), quantise_e)
-            when(sequence_that_starts_at(s - 6), invert_sums)
-            if finished is not None:
-                normalise_and_store(finished, 0)
-                normalise_and_store(finished, 1)
-            when(unit(s + 2), exp_bias)
+            when(unit(s + 1), max_scores)
+            when(sequence_that_starts_at(s - 2), quantise_v)
+            when(pair_that_ends_at(s - 2), quantise_e)
+            when(sequence_that_starts_at(s - 4), invert_sums)
+            when(pair_that_ends_at(s - 5), normalise_and_store)
+            when(sequence_that_starts_at(s + 4), lambda b: copy_k(b, 0, nc.vector.tensor_copy))
+            when(unit(s + 1), exp_bias)
 
             when(unit(s), exponentials)
-            when(unit(s), transpose_e)
-            when(pair_that_ends_at(s - 3), multiply_v)
             when(unit(s - 1), regroup_e)
-            when(sequence_that_starts_at(s + 5), copy_qk)
+            when(sequence_that_starts_at(s + 4), copy_q)
+            when(sequence_that_starts_at(s + 1 if s < 0 else s + 2), lambda b: copy_k(b, 1, nc.scalar.copy))

@@ -64,14 +64,20 @@ def tile_radixattention_s_kernel(tc, q, k, v, k_cache, v_cache, out):
         ident_f32 = consts.tile([P, P], F32, name="ident_f32")
         make_identity(nc, ident_f32[:])
         ident_t = consts.tile([P, P], F32, name="ident_t")
-        nc.vector.tensor_copy(
-            out=ident_t[:].rearrange("p (t r) -> p t r", t=4),
-            in_=ident_f32[:].rearrange("p (r t) -> p t r", t=4),
-        )
         warm_in = consts.tile([P, 1], F32, name="warm_in")
         warm_out = consts.tile([P, 1], F32, name="warm_out")
         nc.vector.memset(warm_in[:], 0.0)
         nc.scalar.activation(out=warm_out[:], in_=warm_in[:], func=ACT.Exp)
+
+        zeros = consts.tile([P, P], F32, name="zeros")
+        nc.vector.memset(zeros[:], 0.0)
+
+        def keep_warm(count):
+            for i in range(count):
+                warm_ps = banks.tile([P, P], F32, name="warm_ps", tag="score", bufs=3)
+                nc.tensor.matmul(out=warm_ps[:], lhsT=zeros[:], rhs=zeros[:], start=True, stop=True)
+
+        keep_warm(4)
 
         q_rows, k_rows, v_rows = {}, {}, {}
         qT_ps, kT_ps, qT, kT = {}, {}, {}, {}
@@ -255,6 +261,11 @@ def tile_radixattention_s_kernel(tc, q, k, v, k_cache, v_cache, out):
                 in_=o_sb[:].rearrange("p a d -> p (a d)"),
             )
 
+        nc.vector.tensor_copy(
+            out=ident_t[:].rearrange("p (t r) -> p t r", t=4),
+            in_=ident_f32[:].rearrange("p (r t) -> p t r", t=4),
+        )
+
         def when(index, stage):
             if index is not None:
                 stage(index)
@@ -275,6 +286,9 @@ def tile_radixattention_s_kernel(tc, q, k, v, k_cache, v_cache, out):
             when(sequence_that_starts_at(s + 5), transpose_q)
             when(sequence_that_starts_at(s + 5), lambda b: transpose_k(b, 0))
             when(sequence_that_starts_at(s + 2 if s < 0 else s + 3), lambda b: transpose_k(b, 1))
+
+            if s == -5:
+                keep_warm(1)
 
             when(unit(s + 1), max_scores)
             when(sequence_that_starts_at(s - 2), quantise_v)

@@ -77,7 +77,7 @@ def tile_radixattention_s_kernel(tc, q, k, v, k_cache, v_cache, out):
                 warm_ps = banks.tile([P, P], F32, name="warm_ps", tag="score", bufs=3)
                 nc.tensor.matmul(out=warm_ps[:], lhsT=zeros[:], rhs=zeros[:], start=True, stop=True)
 
-        keep_warm(4)
+        keep_warm(5)
 
         q_rows, k_rows, v_rows = {}, {}, {}
         qT_ps, kT_ps, qT, kT = {}, {}, {}, {}
@@ -98,20 +98,22 @@ def tile_radixattention_s_kernel(tc, q, k, v, k_cache, v_cache, out):
                 )
 
         def load_qk(b):
-            q_rows[b] = keep.tile([P, H * D], BF16, name="q_rows%d" % b)
-            nc.sync.dma_start(out=q_rows[b][:], in_=q[b].rearrange("e h d -> e (h d)"))
             k_rows[b] = keep.tile([P, 4, HK * D], BF16, name="k_rows%d" % b)
             load_keys(k_rows[b], k_cache[b], k[b])
+            q_rows[b] = keep.tile([P, H * D], BF16, name="q_rows%d" % b)
+            nc.sync.dma_start(out=q_rows[b][:], in_=q[b].rearrange("e h d -> e (h d)"))
 
         def load_v(b):
             v_rows[b] = keep.tile([P, 4, HK * D], BF16, name="v_rows%d" % b)
             load_keys(v_rows[b], v_cache[b], v[b])
 
-        def transpose_q(b):
-            qT_ps[b] = banks.tile([P, H * E], BF16, name="qT_ps", tag="work", bufs=3)
-            for h in range(H):
+        def transpose_q(b, heads):
+            qT_ps[b, heads.start] = banks.tile([P, H * E], BF16, name="qT_ps", tag="work", bufs=3)
+            for h in heads:
                 cols = slice(h * D, (h + 1) * D)
-                nc.tensor.transpose(qT_ps[b][:, cols], q_rows[b][:, cols], ident_bf[:])
+                nc.tensor.transpose(
+                    qT_ps[b, heads.start][:, cols], q_rows[b][:, cols], ident_bf[:]
+                )
 
         def transpose_k(b, g):
             kT_ps[b, g] = banks.tile([P, S], BF16, name="kT_ps", tag="work", bufs=3)
@@ -122,9 +124,11 @@ def tile_radixattention_s_kernel(tc, q, k, v, k_cache, v_cache, out):
                     ident_bf[:],
                 )
 
-        def copy_q(b):
-            qT[b] = keep.tile([P, H * E], BF16, name="qT%d" % b)
-            nc.scalar.copy(out=qT[b][:], in_=qT_ps[b][:])
+        def copy_q(b, heads):
+            if heads.start == 0:
+                qT[b] = keep.tile([P, H * E], BF16, name="qT%d" % b)
+            cols = slice(heads.start * E, heads.stop * E)
+            nc.scalar.copy(out=qT[b][:, cols], in_=qT_ps[b, heads.start][:, cols])
 
         def copy_k(b, g, copy):
             kT[b, g] = keep.tile([P, S], BF16, name="kT%d_%d" % (b, g))
@@ -220,21 +224,24 @@ def tile_radixattention_s_kernel(tc, q, k, v, k_cache, v_cache, out):
                 in_=eT_ps[n][:].rearrange("p u i -> p i u"),
             )
 
-        def quantise_e(p):
-            e_codes[p] = keep.tile([P, G * E], U32, name="e_codes%d" % p, align_bytes=64)
-            e_scales[p] = keep.tile([P, G * E], U8, name="e_scales%d" % p, align_bytes=64)
+        def quantise_e(p, heads):
+            if heads.start == 0:
+                e_codes[p] = keep.tile([P, G * E], U32, name="e_codes%d" % p, align_bytes=64)
+                e_scales[p] = keep.tile([P, G * E], U8, name="e_scales%d" % p, align_bytes=64)
+            cols = slice(heads.start * E, heads.stop * E)
             nc.vector.quantize_mx(
-                out=e_codes[p][:].bitcast(FP8X4),
-                scales=e_scales[p][:],
-                in_=e_grouped[p][:].rearrange("p a c -> p (a c)"),
+                out=e_codes[p][:, cols].bitcast(FP8X4),
+                scales=e_scales[p][:, cols],
+                in_=e_grouped[p][:, heads.start : heads.stop, :].rearrange("p a c -> p (a c)"),
             )
 
-        def multiply_v(p):
+        def multiply_v(p, heads):
             b, g = divmod(p, HK)
-            o_ps[p] = banks.tile([P, G, D], F32, name="o_ps", tag="o", bufs=2)
-            for a in range(G):
+            tag, bufs = ("o", 2) if len(heads) == G else ("score", 3)
+            o_ps[p, heads.start] = banks.tile([P, G, D], F32, name="o_ps", tag=tag, bufs=bufs)
+            for a in heads:
                 nc.tensor.matmul_mx(
-                    out=o_ps[p][:, a, :],
+                    out=o_ps[p, heads.start][:, a, :],
                     lhsT=e_codes[p][:, a * E : (a + 1) * E].bitcast(FP8X4),
                     lhsT_scale=e_scales[p][:, a * E : (a + 1) * E],
                     rhs=v_codes[b][:, g * D : (g + 1) * D].bitcast(FP8X4),
@@ -247,17 +254,19 @@ def tile_radixattention_s_kernel(tc, q, k, v, k_cache, v_cache, out):
             inv_sum[b] = keep.tile([P, H], F32, name="inv_sum%d" % b)
             nc.vector.reciprocal(out=inv_sum[b][:], in_=row_sum[b][:])
 
-        def normalise_and_store(p):
+        def normalise_and_store(p, heads):
             b, g = divmod(p, HK)
-            o_sb = keep.tile([P, G, D], F32, name="o_sb%d" % p)
+            count = len(heads)
+            first = g * G + heads.start
+            o_sb = keep.tile([P, count, D], F32, name="o_sb%d_%d" % (p, heads.start))
             nc.vector.tensor_tensor(
                 out=o_sb[:],
-                in0=o_ps[p][:],
-                in1=inv_sum[b][:, g * G : (g + 1) * G].unsqueeze(2).to_broadcast([P, G, D]),
+                in0=o_ps[p, heads.start][:, heads.start : heads.stop, :],
+                in1=inv_sum[b][:, first : first + count].unsqueeze(2).to_broadcast([P, count, D]),
                 op=ALU.mult,
             )
             nc.sync.dma_start(
-                out=out[b * E : (b + 1) * E, g * G * D : (g + 1) * G * D],
+                out=out[b * E : (b + 1) * E, first * D : (first + count) * D],
                 in_=o_sb[:].rearrange("p a d -> p (a d)"),
             )
 
@@ -273,32 +282,48 @@ def tile_radixattention_s_kernel(tc, q, k, v, k_cache, v_cache, out):
         def unit(n):
             return n if 0 <= n < N_HEADS else None
 
+        def by_pair(n, stage):
+            p, a = divmod(n, G)
+            if p == N_PAIRS - 1:
+                stage(p, range(a, a + 1))
+            elif 0 <= p < N_PAIRS and a == G - 1:
+                stage(p, range(G))
+
+        load_qk(0)
         for b in range(B):
-            load_qk(b)
+            if b + 1 < B:
+                load_qk(b + 1)
             load_v(b)
         for b in range(B):
             regroup_v(b)
 
-        for s in range(-5, N_HEADS + 6):
+        transpose_k(0, 0)
+        copy_k(0, 0, nc.vector.tensor_copy)
+        transpose_q(0, range(1))
+        copy_q(0, range(1))
+        transpose_q(0, range(1, H))
+        copy_q(0, range(1, H))
+        keep_warm(1)
+
+        for s in range(-2, N_HEADS + 5):
             when(unit(s + 2), score)
             when(unit(s - 1), transpose_e)
-            when(pair_that_ends_at(s - 3), multiply_v)
-            when(sequence_that_starts_at(s + 5), transpose_q)
+            by_pair(s - 3, multiply_v)
+            when(sequence_that_starts_at(s + 5), lambda b: transpose_q(b, range(H)))
             when(sequence_that_starts_at(s + 5), lambda b: transpose_k(b, 0))
             when(sequence_that_starts_at(s + 2 if s < 0 else s + 3), lambda b: transpose_k(b, 1))
 
-            if s == -5:
-                keep_warm(1)
-
             when(unit(s + 1), max_scores)
             when(sequence_that_starts_at(s - 2), quantise_v)
-            when(pair_that_ends_at(s - 2), quantise_e)
+            by_pair(s - 2, quantise_e)
             when(sequence_that_starts_at(s - 4), invert_sums)
-            when(pair_that_ends_at(s - 5), normalise_and_store)
-            when(sequence_that_starts_at(s + 4), lambda b: copy_k(b, 0, nc.vector.tensor_copy))
+            by_pair(s - 5, normalise_and_store)
+            if s >= 0:
+                when(sequence_that_starts_at(s + 4), lambda b: copy_k(b, 0, nc.vector.tensor_copy))
             when(unit(s + 1), exp_bias)
 
             when(unit(s), exponentials)
             when(unit(s - 1), regroup_e)
-            when(sequence_that_starts_at(s + 4), copy_q)
+            if s >= 0:
+                when(sequence_that_starts_at(s + 4), lambda b: copy_q(b, range(H)))
             when(sequence_that_starts_at(s + 1 if s < 0 else s + 2), lambda b: copy_k(b, 1, nc.scalar.copy))

@@ -63,7 +63,6 @@ def tile_radixattention_s_kernel(tc, q, k, v, k_cache, v_cache, out):
         )
         ident_f32 = consts.tile([P, P], F32, name="ident_f32")
         make_identity(nc, ident_f32[:])
-        ident_t = consts.tile([P, P], F32, name="ident_t")
         warm_in = consts.tile([P, 1], F32, name="warm_in")
         warm_out = consts.tile([P, 1], F32, name="warm_out")
         nc.vector.memset(warm_in[:], 0.0)
@@ -74,10 +73,10 @@ def tile_radixattention_s_kernel(tc, q, k, v, k_cache, v_cache, out):
 
         def keep_warm(count):
             for i in range(count):
-                warm_ps = banks.tile([P, P], F32, name="warm_ps", tag="score", bufs=3)
+                warm_ps = banks.tile([P, P], F32, name="warm_ps", tag="o", bufs=2)
                 nc.tensor.matmul(out=warm_ps[:], lhsT=zeros[:], rhs=zeros[:], start=True, stop=True)
 
-        keep_warm(5)
+        keep_warm(4)
 
         q_rows, k_rows, v_rows = {}, {}, {}
         qT_ps, kT_ps, qT, kT = {}, {}, {}, {}
@@ -86,26 +85,41 @@ def tile_radixattention_s_kernel(tc, q, k, v, k_cache, v_cache, out):
         score_ps, e_rows = {}, {}
         eT_ps, e_grouped, e_codes, e_scales, o_ps = {}, {}, {}, {}, {}
 
-        def load_keys(rows, cached, extend):
+        def load_k(b):
+            k_rows[b] = keep.tile([P, S // P, HK * D], BF16, name="k_rows%d" % b)
+            nc.sync.dma_start(
+                out=k_rows[b][:, 0 : PREFIX // P, :],
+                in_=k_cache[b].rearrange("(t p) g d -> p t (g d)", p=P),
+            )
+            nc.sync.dma_start(
+                out=k_rows[b][:, PREFIX // P, :], in_=k[b].rearrange("e g d -> e (g d)")
+            )
+
+        def load_q(sequences):
+            rows = keep.tile([P, len(sequences), H * D], BF16, name="q_rows%d" % sequences.start)
+            nc.sync.dma_start(
+                out=rows[:],
+                in_=q[sequences.start : sequences.stop].rearrange("b e h d -> e b (h d)"),
+            )
+            for i, b in enumerate(sequences):
+                q_rows[b] = rows[:, i, :]
+
+        def load_v(sequences):
+            rows = keep.tile(
+                [P, len(sequences), 4 * HK * D], BF16, name="v_rows%d" % sequences.start
+            )
+            span = slice(sequences.start, sequences.stop)
             for partitions, source in (
-                (slice(0, 64), cached[0:256]),
-                (slice(64, 96), cached[256:PREFIX]),
-                (slice(96, P), extend),
+                (slice(0, 64), v_cache[span, 0:256]),
+                (slice(64, 96), v_cache[span, 256:PREFIX]),
+                (slice(96, P), v[span]),
             ):
                 nc.sync.dma_start(
-                    out=rows[partitions].rearrange("p t c -> p (t c)"),
-                    in_=source.rearrange("(p t) g d -> p (t g d)", t=4),
+                    out=rows[partitions],
+                    in_=source.rearrange("b (p t) g d -> p b (t g d)", t=4),
                 )
-
-        def load_qk(b):
-            k_rows[b] = keep.tile([P, 4, HK * D], BF16, name="k_rows%d" % b)
-            load_keys(k_rows[b], k_cache[b], k[b])
-            q_rows[b] = keep.tile([P, H * D], BF16, name="q_rows%d" % b)
-            nc.sync.dma_start(out=q_rows[b][:], in_=q[b].rearrange("e h d -> e (h d)"))
-
-        def load_v(b):
-            v_rows[b] = keep.tile([P, 4, HK * D], BF16, name="v_rows%d" % b)
-            load_keys(v_rows[b], v_cache[b], v[b])
+            for i, b in enumerate(sequences):
+                v_rows[b] = rows[:, i, :]
 
         def transpose_q(b, heads):
             qT_ps[b, heads.start] = banks.tile([P, H * E], BF16, name="qT_ps", tag="work", bufs=3)
@@ -140,7 +154,7 @@ def tile_radixattention_s_kernel(tc, q, k, v, k_cache, v_cache, out):
             )
             nc.gpsimd.tensor_scalar(
                 out=v_grouped[b][:],
-                in0=v_rows[b][:].rearrange("p t c -> p c t"),
+                in0=v_rows[b].rearrange("p (t c) -> p c t", t=4),
                 scalar1=1.0,
                 scalar2=0.0,
                 op0=ALU.mult,
@@ -171,9 +185,9 @@ def tile_radixattention_s_kernel(tc, q, k, v, k_cache, v_cache, out):
                 stop=False,
             )
             nc.tensor.matmul(
-                out=score_ps[n][:].rearrange("p (t j) -> p t j", t=4)[:, :, PREFIX // 4 : P],
+                out=score_ps[n][:, PREFIX:S],
                 lhsT=hidden_t[:],
-                rhs=ident_t[:],
+                rhs=ident_f32[:],
                 is_transpose=True,
                 start=False,
                 stop=True,
@@ -200,7 +214,7 @@ def tile_radixattention_s_kernel(tc, q, k, v, k_cache, v_cache, out):
             e_rows[n] = keep.tile([P, S], BF16, name="e_rows%d" % n)
             nc.scalar.activation(
                 out=e_rows[n][:].rearrange("p (u j x) -> p u j x", u=2, x=2),
-                in_=score_ps[n][:].rearrange("p (u x j) -> p u j x", u=2, x=2),
+                in_=score_ps[n][:].rearrange("p (j u x) -> p u j x", u=2, x=2),
                 func=ACT.Exp,
                 bias=neg_max[b][:, h : h + 1],
                 scale=SCALING,
@@ -270,11 +284,6 @@ def tile_radixattention_s_kernel(tc, q, k, v, k_cache, v_cache, out):
                 in_=o_sb[:].rearrange("p a d -> p (a d)"),
             )
 
-        nc.vector.tensor_copy(
-            out=ident_t[:].rearrange("p (t r) -> p t r", t=4),
-            in_=ident_f32[:].rearrange("p (r t) -> p t r", t=4),
-        )
-
         def when(index, stage):
             if index is not None:
                 stage(index)
@@ -289,11 +298,16 @@ def tile_radixattention_s_kernel(tc, q, k, v, k_cache, v_cache, out):
             elif 0 <= p < N_PAIRS and a == G - 1:
                 stage(p, range(G))
 
-        load_qk(0)
-        for b in range(B):
-            if b + 1 < B:
-                load_qk(b + 1)
-            load_v(b)
+        load_k(0)
+        load_q(range(1))
+        load_v(range(1))
+        load_k(1)
+        load_q(range(1, 2))
+        load_v(range(1, 2))
+        load_k(2)
+        load_k(3)
+        load_q(range(2, B))
+        load_v(range(2, B))
         for b in range(B):
             regroup_v(b)
 
@@ -303,7 +317,7 @@ def tile_radixattention_s_kernel(tc, q, k, v, k_cache, v_cache, out):
         copy_q(0, range(1))
         transpose_q(0, range(1, H))
         copy_q(0, range(1, H))
-        keep_warm(1)
+        keep_warm(2)
 
         for s in range(-2, N_HEADS + 5):
             when(unit(s + 2), score)

@@ -11,7 +11,6 @@ U8 = mybir.dt.uint8
 FP8X4 = mybir.dt.float8_e4m3fn_x4
 ALU = mybir.AluOpType
 ACT = mybir.ActivationFunctionType
-AX = mybir.AxisListType
 
 B = 4
 E = 128
@@ -76,12 +75,12 @@ def tile_radixattention_s_kernel(tc, q, k, v, k_cache, v_cache, out):
                 warm_ps = banks.tile([P, P], F32, name="warm_ps", tag="o", bufs=2)
                 nc.tensor.matmul(out=warm_ps[:], lhsT=zeros[:], rhs=zeros[:], start=True, stop=True)
 
-        keep_warm(4)
+        keep_warm(5)
 
         q_rows, k_rows, v_rows = {}, {}, {}
         qT_ps, kT_ps, qT, kT = {}, {}, {}, {}
         v_grouped, v_codes, v_scales = {}, {}, {}
-        row_max, neg_max, row_sum, inv_sum = {}, {}, {}, {}
+        neg_max, row_sum, inv_sum = {}, {}, {}
         score_ps, e_rows = {}, {}
         eT_ps, e_grouped, e_codes, e_scales, o_ps = {}, {}, {}, {}, {}
 
@@ -173,7 +172,6 @@ def tile_radixattention_s_kernel(tc, q, k, v, k_cache, v_cache, out):
         def score(n):
             b, h = divmod(n, H)
             if h == 0:
-                row_max[b] = keep.tile([P, H], F32, name="row_max%d" % b)
                 neg_max[b] = keep.tile([P, H], F32, name="neg_max%d" % b)
                 row_sum[b] = keep.tile([P, H], F32, name="row_sum%d" % b)
             score_ps[n] = banks.tile([P, S], F32, name="score_ps", tag="score", bufs=3)
@@ -195,23 +193,19 @@ def tile_radixattention_s_kernel(tc, q, k, v, k_cache, v_cache, out):
 
         def max_scores(n):
             b, h = divmod(n, H)
-            nc.vector.tensor_reduce(
-                out=row_max[b][:, h : h + 1], in_=score_ps[n][:], axis=AX.X, op=ALU.max
-            )
-
-        def exp_bias(n):
-            b, h = divmod(n, H)
+            e_rows[n] = keep.tile([P, S], BF16, name="e_rows%d" % n)
             nc.vector.tensor_scalar(
-                out=neg_max[b][:, h : h + 1],
-                in0=row_max[b][:, h : h + 1],
+                out=e_rows[n][:],
+                in0=score_ps[n][:],
                 scalar1=-SCALING,
                 scalar2=None,
                 op0=ALU.mult,
+                op1=ALU.min,
+                accum_out=neg_max[b][:, h : h + 1],
             )
 
         def exponentials(n):
             b, h = divmod(n, H)
-            e_rows[n] = keep.tile([P, S], BF16, name="e_rows%d" % n)
             nc.scalar.activation(
                 out=e_rows[n][:].rearrange("p (u j x) -> p u j x", u=2, x=2),
                 in_=score_ps[n][:].rearrange("p (j u x) -> p u j x", u=2, x=2),
@@ -300,9 +294,9 @@ def tile_radixattention_s_kernel(tc, q, k, v, k_cache, v_cache, out):
 
         load_k(0)
         load_q(range(1))
-        load_v(range(1))
         load_k(1)
         load_q(range(1, 2))
+        load_v(range(1))
         load_v(range(1, 2))
         load_k(2)
         load_k(3)
@@ -317,7 +311,7 @@ def tile_radixattention_s_kernel(tc, q, k, v, k_cache, v_cache, out):
         copy_q(0, range(1))
         transpose_q(0, range(1, H))
         copy_q(0, range(1, H))
-        keep_warm(2)
+        keep_warm(1)
 
         for s in range(-2, N_HEADS + 5):
             when(unit(s + 2), score)
@@ -334,7 +328,6 @@ def tile_radixattention_s_kernel(tc, q, k, v, k_cache, v_cache, out):
             by_pair(s - 5, normalise_and_store)
             if s >= 0:
                 when(sequence_that_starts_at(s + 4), lambda b: copy_k(b, 0, nc.vector.tensor_copy))
-            when(unit(s + 1), exp_bias)
 
             when(unit(s), exponentials)
             when(unit(s - 1), regroup_e)

@@ -297,11 +297,13 @@ def tile_radixattention_s_kernel(tc, q, k, v, k_cache, v_cache, out):
         load_k(1)
         load_q(range(1, 2))
         load_v(range(1))
-        load_v(range(1, 2))
         load_k(2)
+        load_q(range(2, 3))
+        load_v(range(1, 2))
         load_k(3)
-        load_q(range(2, B))
-        load_v(range(2, B))
+        load_q(range(3, 4))
+        load_v(range(2, 3))
+        load_v(range(3, 4))
         for b in range(B):
             regroup_v(b)
 

@@ -67,6 +67,28 @@ def tile_radixattention_s_kernel(tc, q, k, v, k_cache, v_cache, out):
         nc.vector.memset(warm_in[:], 0.0)
         nc.scalar.activation(out=warm_out[:], in_=warm_in[:], func=ACT.Exp)
 
+        zeros_bf = consts.tile([P, 1024], BF16, name="zeros_bf", align_bytes=64)
+        nc.vector.memset(zeros_bf[:], 0.0)
+        zero_codes = consts.tile([P, 256], U32, name="zero_codes", align_bytes=64)
+        zero_scales = consts.tile([P, 256], U8, name="zero_scales", align_bytes=64)
+        nc.vector.quantize_mx(
+            out=zero_codes[:].bitcast(FP8X4), scales=zero_scales[:], in_=zeros_bf[:]
+        )
+
+        def warm_mx(count):
+            for i in range(count):
+                warm_ps = banks.tile([P, G, HK * D], F32, name="warm_ps", tag="o", bufs=2)
+                nc.tensor.matmul_mx(
+                    out=warm_ps[:, 0, :],
+                    lhsT=zero_codes[:, 0:P].bitcast(FP8X4),
+                    lhsT_scale=zero_scales[:, 0:P],
+                    rhs=zero_codes[:].bitcast(FP8X4),
+                    rhs_scale=zero_scales[:],
+                    start=True,
+                    stop=True,
+                )
+
+        warm_mx(10)
         zeros = consts.tile([P, P], F32, name="zeros")
         nc.vector.memset(zeros[:], 0.0)
 
@@ -74,8 +96,6 @@ def tile_radixattention_s_kernel(tc, q, k, v, k_cache, v_cache, out):
             for i in range(count):
                 warm_ps = banks.tile([P, P], F32, name="warm_ps", tag="o", bufs=2)
                 nc.tensor.matmul(out=warm_ps[:], lhsT=zeros[:], rhs=zeros[:], start=True, stop=True)
-
-        keep_warm(5)
 
         q_rows, k_rows, v_rows = {}, {}, {}
         qT_ps, kT_ps, qT, kT = {}, {}, {}, {}
@@ -246,14 +266,14 @@ def tile_radixattention_s_kernel(tc, q, k, v, k_cache, v_cache, out):
         def multiply_v(p, heads):
             b, g = divmod(p, HK)
             tag, bufs = ("o", 2) if len(heads) == G else ("score", 3)
-            o_ps[p, heads.start] = banks.tile([P, G, D], F32, name="o_ps", tag=tag, bufs=bufs)
+            o_ps[p, heads.start] = banks.tile([P, G, HK * D], F32, name="o_ps", tag=tag, bufs=bufs)
             for a in heads:
                 nc.tensor.matmul_mx(
                     out=o_ps[p, heads.start][:, a, :],
                     lhsT=e_codes[p][:, a * E : (a + 1) * E].bitcast(FP8X4),
                     lhsT_scale=e_scales[p][:, a * E : (a + 1) * E],
-                    rhs=v_codes[b][:, g * D : (g + 1) * D].bitcast(FP8X4),
-                    rhs_scale=v_scales[b][:, g * D : (g + 1) * D],
+                    rhs=v_codes[b][:].bitcast(FP8X4),
+                    rhs_scale=v_scales[b][:],
                     start=True,
                     stop=True,
                 )
@@ -269,7 +289,7 @@ def tile_radixattention_s_kernel(tc, q, k, v, k_cache, v_cache, out):
             o_sb = keep.tile([P, count, D], F32, name="o_sb%d_%d" % (p, heads.start))
             nc.vector.tensor_tensor(
                 out=o_sb[:],
-                in0=o_ps[p, heads.start][:, heads.start : heads.stop, :],
+                in0=o_ps[p, heads.start][:, heads.start : heads.stop, g * D : (g + 1) * D],
                 in1=inv_sum[b][:, first : first + count].unsqueeze(2).to_broadcast([P, count, D]),
                 op=ALU.mult,
             )
@@ -316,6 +336,8 @@ def tile_radixattention_s_kernel(tc, q, k, v, k_cache, v_cache, out):
         keep_warm(1)
 
         for s in range(-2, N_HEADS + 5):
+            if s < 1:
+                warm_mx(1)
             when(unit(s + 2), score)
             when(unit(s - 1), transpose_e)
             by_pair(s - 3, multiply_v)

@@ -67,35 +67,40 @@ def tile_radixattention_s_kernel(tc, q, k, v, k_cache, v_cache, out):
         nc.vector.memset(warm_in[:], 0.0)
         nc.scalar.activation(out=warm_out[:], in_=warm_in[:], func=ACT.Exp)
 
-        zeros_bf = consts.tile([P, 1024], BF16, name="zeros_bf", align_bytes=64)
-        nc.vector.memset(zeros_bf[:], 0.0)
-        zero_codes = consts.tile([P, 256], U32, name="zero_codes", align_bytes=64)
-        zero_scales = consts.tile([P, 256], U8, name="zero_scales", align_bytes=64)
+        zeros = consts.tile([P, 2 * P], F32, name="zeros", align_bytes=64)
+        nc.vector.memset(zeros[:], 0.0)
+        zero_codes = consts.tile([P, P], U32, name="zero_codes", align_bytes=64)
+        zero_scales = consts.tile([P, P], U8, name="zero_scales", align_bytes=64)
         nc.vector.quantize_mx(
-            out=zero_codes[:].bitcast(FP8X4), scales=zero_scales[:], in_=zeros_bf[:]
+            out=zero_codes[:].bitcast(FP8X4), scales=zero_scales[:], in_=zeros[:].bitcast(BF16)
         )
 
-        def warm_mx(count):
+        def keep_warm(count):
+            for i in range(count):
+                warm_ps = banks.tile([P, G, HK * D], F32, name="warm_ps", tag="o", bufs=2)
+                nc.tensor.matmul(
+                    out=warm_ps[:, 0, 0:P],
+                    lhsT=zeros[:, 0:P],
+                    rhs=zeros[:, 0:P],
+                    start=True,
+                    stop=True,
+                )
+
+        def keep_warm_mx(count):
             for i in range(count):
                 warm_ps = banks.tile([P, G, HK * D], F32, name="warm_ps", tag="o", bufs=2)
                 nc.tensor.matmul_mx(
-                    out=warm_ps[:, 0, :],
-                    lhsT=zero_codes[:, 0:P].bitcast(FP8X4),
-                    lhsT_scale=zero_scales[:, 0:P],
+                    out=warm_ps[:, 0, 0:P],
+                    lhsT=zero_codes[:].bitcast(FP8X4),
+                    lhsT_scale=zero_scales[:],
                     rhs=zero_codes[:].bitcast(FP8X4),
                     rhs_scale=zero_scales[:],
                     start=True,
                     stop=True,
                 )
 
-        warm_mx(10)
-        zeros = consts.tile([P, P], F32, name="zeros")
-        nc.vector.memset(zeros[:], 0.0)
-
-        def keep_warm(count):
-            for i in range(count):
-                warm_ps = banks.tile([P, P], F32, name="warm_ps", tag="o", bufs=2)
-                nc.tensor.matmul(out=warm_ps[:], lhsT=zeros[:], rhs=zeros[:], start=True, stop=True)
+        keep_warm(4)
+        keep_warm_mx(8)
 
         q_rows, k_rows, v_rows = {}, {}, {}
         qT_ps, kT_ps, qT, kT = {}, {}, {}, {}
@@ -336,9 +341,9 @@ def tile_radixattention_s_kernel(tc, q, k, v, k_cache, v_cache, out):
         keep_warm(1)
 
         for s in range(-2, N_HEADS + 5):
-            if s < 1:
-                warm_mx(1)
             when(unit(s + 2), score)
+            if s == -2:
+                keep_warm(1)
             when(unit(s - 1), transpose_e)
             by_pair(s - 3, multiply_v)
             when(sequence_that_starts_at(s + 5), lambda b: transpose_q(b, range(H)))

@@ -67,40 +67,15 @@ def tile_radixattention_s_kernel(tc, q, k, v, k_cache, v_cache, out):
         nc.vector.memset(warm_in[:], 0.0)
         nc.scalar.activation(out=warm_out[:], in_=warm_in[:], func=ACT.Exp)
 
-        zeros = consts.tile([P, 2 * P], F32, name="zeros", align_bytes=64)
+        zeros = consts.tile([P, P], F32, name="zeros")
         nc.vector.memset(zeros[:], 0.0)
-        zero_codes = consts.tile([P, P], U32, name="zero_codes", align_bytes=64)
-        zero_scales = consts.tile([P, P], U8, name="zero_scales", align_bytes=64)
-        nc.vector.quantize_mx(
-            out=zero_codes[:].bitcast(FP8X4), scales=zero_scales[:], in_=zeros[:].bitcast(BF16)
-        )
 
         def keep_warm(count):
             for i in range(count):
-                warm_ps = banks.tile([P, G, HK * D], F32, name="warm_ps", tag="o", bufs=2)
-                nc.tensor.matmul(
-                    out=warm_ps[:, 0, 0:P],
-                    lhsT=zeros[:, 0:P],
-                    rhs=zeros[:, 0:P],
-                    start=True,
-                    stop=True,
-                )
-
-        def keep_warm_mx(count):
-            for i in range(count):
-                warm_ps = banks.tile([P, G, HK * D], F32, name="warm_ps", tag="o", bufs=2)
-                nc.tensor.matmul_mx(
-                    out=warm_ps[:, 0, 0:P],
-                    lhsT=zero_codes[:].bitcast(FP8X4),
-                    lhsT_scale=zero_scales[:],
-                    rhs=zero_codes[:].bitcast(FP8X4),
-                    rhs_scale=zero_scales[:],
-                    start=True,
-                    stop=True,
-                )
+                warm_ps = banks.tile([P, P], F32, name="warm_ps", tag="o", bufs=2)
+                nc.tensor.matmul(out=warm_ps[:], lhsT=zeros[:], rhs=zeros[:], start=True, stop=True)
 
         keep_warm(4)
-        keep_warm_mx(8)
 
         q_rows, k_rows, v_rows = {}, {}, {}
         qT_ps, kT_ps, qT, kT = {}, {}, {}, {}

@@ -151,14 +151,18 @@ def tile_radixattention_s_kernel(tc, q, k, v, k_cache, v_cache, out):
             v_grouped[b] = keep.tile(
                 [P, HK * D, 4], BF16, name="v_grouped%d" % b, align_bytes=64
             )
-            nc.gpsimd.tensor_scalar(
-                out=v_grouped[b][:],
-                in0=v_rows[b].rearrange("p (t c) -> p c t", t=4),
-                scalar1=1.0,
-                scalar2=0.0,
-                op0=ALU.mult,
-                op1=ALU.add,
-            )
+            rows = v_rows[b].rearrange("p (t c) -> p c t", t=4)
+            width = HK * D // 4
+            for first in range(0, HK * D, width):
+                cols = slice(first, first + width)
+                nc.gpsimd.tensor_scalar(
+                    out=v_grouped[b][:, cols, :],
+                    in0=rows[:, cols, :],
+                    scalar1=1.0,
+                    scalar2=0.0,
+                    op0=ALU.mult,
+                    op1=ALU.add,
+                )
 
         def quantise_v(b):
             v_codes[b] = keep.tile([P, HK * D], U32, name="v_codes%d" % b, align_bytes=64)
@@ -297,13 +301,12 @@ def tile_radixattention_s_kernel(tc, q, k, v, k_cache, v_cache, out):
         load_k(1)
         load_q(range(1, 2))
         load_v(range(1))
+        load_v(range(1, 2))
         load_k(2)
         load_q(range(2, 3))
-        load_v(range(1, 2))
+        load_v(range(2, B))
         load_k(3)
         load_q(range(3, 4))
-        load_v(range(2, 3))
-        load_v(range(3, 4))
         for b in range(B):
             regroup_v(b)
 

@@ -22,6 +22,7 @@ G = H // HK
 D = 128
 P = 128
 SCALING = 1.0 / math.sqrt(D)
+SHIFT = 3 * math.log(2.0)
 HIDDEN = -1.0e30
 
 FLOPS = 2 * 2 * B * H * E * S * D
@@ -80,7 +81,7 @@ def tile_radixattention_s_kernel(tc, q, k, v, k_cache, v_cache, out):
         q_rows, k_rows, v_rows = {}, {}, {}
         qT_ps, kT_ps, qT, kT = {}, {}, {}, {}
         v_grouped, v_codes, v_scales = {}, {}, {}
-        neg_max, row_sum, inv_sum = {}, {}, {}
+        neg_max, exp_bias, row_sum, inv_sum = {}, {}, {}, {}
         score_ps, e_rows = {}, {}
         eT_ps, e_grouped, e_codes, e_scales, o_ps = {}, {}, {}, {}, {}
 
@@ -177,6 +178,7 @@ def tile_radixattention_s_kernel(tc, q, k, v, k_cache, v_cache, out):
             b, h = divmod(n, H)
             if h == 0:
                 neg_max[b] = keep.tile([P, H], F32, name="neg_max%d" % b)
+                exp_bias[b] = keep.tile([P, H], F32, name="exp_bias%d" % b)
                 row_sum[b] = keep.tile([P, H], F32, name="row_sum%d" % b)
             score_ps[n] = banks.tile([P, S], F32, name="score_ps", tag="score", bufs=3)
             nc.tensor.matmul(
@@ -207,6 +209,13 @@ def tile_radixattention_s_kernel(tc, q, k, v, k_cache, v_cache, out):
                 op1=ALU.min,
                 accum_out=neg_max[b][:, h : h + 1],
             )
+            nc.vector.tensor_scalar(
+                out=exp_bias[b][:, h : h + 1],
+                in0=neg_max[b][:, h : h + 1],
+                scalar1=SHIFT,
+                scalar2=None,
+                op0=ALU.add,
+            )
 
         def exponentials(n):
             b, h = divmod(n, H)
@@ -214,7 +223,7 @@ def tile_radixattention_s_kernel(tc, q, k, v, k_cache, v_cache, out):
                 out=e_rows[n][:].rearrange("p (u j x) -> p u j x", u=2, x=2),
                 in_=score_ps[n][:].rearrange("p (j u x) -> p u j x", u=2, x=2),
                 func=ACT.Exp,
-                bias=neg_max[b][:, h : h + 1],
+                bias=exp_bias[b][:, h : h + 1],
                 scale=SCALING,
                 accum_out=row_sum[b][:, h : h + 1],
             )

@@ -11,6 +11,7 @@ U8 = mybir.dt.uint8
 FP8X4 = mybir.dt.float8_e4m3fn_x4
 ALU = mybir.AluOpType
 ACT = mybir.ActivationFunctionType
+AXIS = mybir.AxisListType
 
 B = 4
 E = 128
@@ -81,7 +82,7 @@ def tile_radixattention_s_kernel(tc, q, k, v, k_cache, v_cache, out):
         q_rows, k_rows, v_rows = {}, {}, {}
         qT_ps, kT_ps, qT, kT = {}, {}, {}, {}
         v_grouped, v_codes, v_scales = {}, {}, {}
-        neg_max, exp_bias, row_sum, inv_sum = {}, {}, {}, {}
+        row_max, exp_bias, row_sum, inv_sum = {}, {}, {}, {}
         score_ps, e_rows = {}, {}
         eT_ps, e_grouped, e_codes, e_scales, o_ps = {}, {}, {}, {}, {}
 
@@ -148,14 +149,15 @@ def tile_radixattention_s_kernel(tc, q, k, v, k_cache, v_cache, out):
             kT[b, g] = keep.tile([P, S], BF16, name="kT%d_%d" % (b, g))
             copy(out=kT[b, g][:], in_=kT_ps[b, g][:])
 
-        def regroup_v(b):
-            v_grouped[b] = keep.tile(
-                [P, HK * D, 4], BF16, name="v_grouped%d" % b, align_bytes=64
-            )
+        def regroup_v(b, part):
+            if part == 0:
+                v_grouped[b] = keep.tile(
+                    [P, HK * D, 4], BF16, name="v_grouped%d" % b, align_bytes=64
+                )
             rows = v_rows[b].rearrange("p (t c) -> p c t", t=4)
             width = HK * D // 4
-            for first in range(0, HK * D, width):
-                cols = slice(first, first + width)
+            for i in range(2 * part, 2 * part + 2):
+                cols = slice(i * width, (i + 1) * width)
                 nc.gpsimd.tensor_scalar(
                     out=v_grouped[b][:, cols, :],
                     in0=rows[:, cols, :],
@@ -177,7 +179,7 @@ def tile_radixattention_s_kernel(tc, q, k, v, k_cache, v_cache, out):
         def score(n):
             b, h = divmod(n, H)
             if h == 0:
-                neg_max[b] = keep.tile([P, H], F32, name="neg_max%d" % b)
+                row_max[b] = keep.tile([P, H], F32, name="row_max%d" % b)
                 exp_bias[b] = keep.tile([P, H], F32, name="exp_bias%d" % b)
                 row_sum[b] = keep.tile([P, H], F32, name="row_sum%d" % b)
             score_ps[n] = banks.tile([P, S], F32, name="score_ps", tag="score", bufs=3)
@@ -199,26 +201,24 @@ def tile_radixattention_s_kernel(tc, q, k, v, k_cache, v_cache, out):
 
         def max_scores(n):
             b, h = divmod(n, H)
-            e_rows[n] = keep.tile([P, S], BF16, name="e_rows%d" % n)
-            nc.vector.tensor_scalar(
-                out=e_rows[n][:],
-                in0=score_ps[n][:],
-                scalar1=-SCALING,
-                scalar2=None,
-                op0=ALU.mult,
-                op1=ALU.min,
-                accum_out=neg_max[b][:, h : h + 1],
+            nc.vector.tensor_reduce(
+                out=row_max[b][:, h : h + 1], in_=score_ps[n][:], axis=AXIS.X, op=ALU.max
             )
-            nc.vector.tensor_scalar(
+
+        def bias_of_exp(n):
+            b, h = divmod(n, H)
+            nc.gpsimd.tensor_scalar(
                 out=exp_bias[b][:, h : h + 1],
-                in0=neg_max[b][:, h : h + 1],
-                scalar1=SHIFT,
-                scalar2=None,
-                op0=ALU.add,
+                in0=row_max[b][:, h : h + 1],
+                scalar1=-SCALING,
+                scalar2=SHIFT,
+                op0=ALU.mult,
+                op1=ALU.add,
             )
 
         def exponentials(n):
             b, h = divmod(n, H)
+            e_rows[n] = keep.tile([P, S], BF16, name="e_rows%d" % n)
             nc.scalar.activation(
                 out=e_rows[n][:].rearrange("p (u j x) -> p u j x", u=2, x=2),
                 in_=score_ps[n][:].rearrange("p (j u x) -> p u j x", u=2, x=2),
@@ -316,8 +316,6 @@ def tile_radixattention_s_kernel(tc, q, k, v, k_cache, v_cache, out):
         load_v(range(2, B))
         load_k(3)
         load_q(range(3, 4))
-        for b in range(B):
-            regroup_v(b)
 
         transpose_k(0, 0)
         copy_k(0, 0, nc.vector.tensor_copy)
@@ -338,7 +336,14 @@ def tile_radixattention_s_kernel(tc, q, k, v, k_cache, v_cache, out):
             when(sequence_that_starts_at(s + 2 if s < 0 else s + 3), lambda b: transpose_k(b, 1))
 
             when(unit(s + 1), max_scores)
-            when(sequence_that_starts_at(s - 2), quantise_v)
+            when(unit(s + 1), bias_of_exp)
+            if s < H // 2:
+                when(sequence_that_starts_at(s), lambda b: regroup_v(b, 0))
+                when(sequence_that_starts_at(s - 1), lambda b: regroup_v(b, 1))
+            else:
+                when(sequence_that_starts_at(s + 2), lambda b: regroup_v(b, 0))
+                when(sequence_that_starts_at(s), lambda b: regroup_v(b, 1))
+            when(sequence_that_starts_at(s - 3), quantise_v)
             by_pair(s - 2, quantise_e)
             when(sequence_that_starts_at(s - 4), invert_sums)
             by_pair(s - 5, normalise_and_store)

@@ -207,7 +207,7 @@ def tile_radixattention_s_kernel(tc, q, k, v, k_cache, v_cache, out):
 
         def bias_of_exp(n):
             b, h = divmod(n, H)
-            nc.gpsimd.tensor_scalar(
+            nc.vector.tensor_scalar(
                 out=exp_bias[b][:, h : h + 1],
                 in0=row_max[b][:, h : h + 1],
                 scalar1=-SCALING,
@@ -317,6 +317,10 @@ def tile_radixattention_s_kernel(tc, q, k, v, k_cache, v_cache, out):
         load_k(3)
         load_q(range(3, 4))
 
+        for b in range(B):
+            regroup_v(b, 0)
+            regroup_v(b, 1)
+
         transpose_k(0, 0)
         copy_k(0, 0, nc.vector.tensor_copy)
         transpose_q(0, range(1))
@@ -336,17 +340,11 @@ def tile_radixattention_s_kernel(tc, q, k, v, k_cache, v_cache, out):
             when(sequence_that_starts_at(s + 2 if s < 0 else s + 3), lambda b: transpose_k(b, 1))
 
             when(unit(s + 1), max_scores)
-            when(unit(s + 1), bias_of_exp)
-            if s < H // 2:
-                when(sequence_that_starts_at(s), lambda b: regroup_v(b, 0))
-                when(sequence_that_starts_at(s - 1), lambda b: regroup_v(b, 1))
-            else:
-                when(sequence_that_starts_at(s + 2), lambda b: regroup_v(b, 0))
-                when(sequence_that_starts_at(s), lambda b: regroup_v(b, 1))
-            when(sequence_that_starts_at(s - 3), quantise_v)
+            when(sequence_that_starts_at(s - 2), quantise_v)
             by_pair(s - 2, quantise_e)
             when(sequence_that_starts_at(s - 4), invert_sums)
             by_pair(s - 5, normalise_and_store)
+            when(unit(s + 1), bias_of_exp)
             if s >= 0:
                 when(sequence_that_starts_at(s + 4), lambda b: copy_k(b, 0, nc.vector.tensor_copy))
 

@@ -86,14 +86,17 @@ def tile_radixattention_s_kernel(tc, q, k, v, k_cache, v_cache, out):
         score_ps, e_rows = {}, {}
         eT_ps, e_grouped, e_codes, e_scales, o_ps = {}, {}, {}, {}, {}
 
-        def load_k(b):
-            k_rows[b] = keep.tile([P, S // P, HK * D], BF16, name="k_rows%d" % b)
+        def load_k(b, heads=range(HK)):
+            if heads.start == 0:
+                k_rows[b] = keep.tile([P, S // P, HK * D], BF16, name="k_rows%d" % b)
+            cols = slice(heads.start * D, heads.stop * D)
+            span = slice(heads.start, heads.stop)
             nc.sync.dma_start(
-                out=k_rows[b][:, 0 : PREFIX // P, :],
-                in_=k_cache[b].rearrange("(t p) g d -> p t (g d)", p=P),
+                out=k_rows[b][:, 0 : PREFIX // P, cols],
+                in_=k_cache[b, :, span].rearrange("(t p) g d -> p t (g d)", p=P),
             )
             nc.sync.dma_start(
-                out=k_rows[b][:, PREFIX // P, :], in_=k[b].rearrange("e g d -> e (g d)")
+                out=k_rows[b][:, PREFIX // P, cols], in_=k[b, :, span].rearrange("e g d -> e (g d)")
             )
 
         def load_q(sequences):
@@ -305,8 +308,9 @@ def tile_radixattention_s_kernel(tc, q, k, v, k_cache, v_cache, out):
             elif 0 <= p < N_PAIRS and a == G - 1:
                 stage(p, range(G))
 
-        load_k(0)
+        load_k(0, range(1))
         load_q(range(1))
+        load_k(0, range(1, HK))
         load_k(1)
         load_q(range(1, 2))
         load_v(range(1))
@@ -340,11 +344,11 @@ def tile_radixattention_s_kernel(tc, q, k, v, k_cache, v_cache, out):
             when(sequence_that_starts_at(s + 2 if s < 0 else s + 3), lambda b: transpose_k(b, 1))
 
             when(unit(s + 1), max_scores)
-            when(sequence_that_starts_at(s - 2), quantise_v)
             by_pair(s - 2, quantise_e)
             when(sequence_that_starts_at(s - 4), invert_sums)
             by_pair(s - 5, normalise_and_store)
             when(unit(s + 1), bias_of_exp)
+            when(sequence_that_starts_at(s - 3), quantise_v)
             if s >= 0:
                 when(sequence_that_starts_at(s + 4), lambda b: copy_k(b, 0, nc.vector.tensor_copy))
 

@@ -263,13 +263,14 @@ def tile_radixattention_s_kernel(tc, q, k, v, k_cache, v_cache, out):
             b, g = divmod(p, HK)
             tag, bufs = ("o", 2) if len(heads) == G else ("score", 3)
             o_ps[p, heads.start] = banks.tile([P, G, HK * D], F32, name="o_ps", tag=tag, bufs=bufs)
+            v_cols = slice(0, HK * D) if len(heads) == G else slice(g * D, (g + 1) * D)
             for a in heads:
                 nc.tensor.matmul_mx(
-                    out=o_ps[p, heads.start][:, a, :],
+                    out=o_ps[p, heads.start][:, a, v_cols],
                     lhsT=e_codes[p][:, a * E : (a + 1) * E].bitcast(FP8X4),
                     lhsT_scale=e_scales[p][:, a * E : (a + 1) * E],
-                    rhs=v_codes[b][:].bitcast(FP8X4),
-                    rhs_scale=v_scales[b][:],
+                    rhs=v_codes[b][:, v_cols].bitcast(FP8X4),
+                    rhs_scale=v_scales[b][:, v_cols],
                     start=True,
                     stop=True,
                 )
@@ -313,11 +314,11 @@ def tile_radixattention_s_kernel(tc, q, k, v, k_cache, v_cache, out):
         load_k(0, range(1, HK))
         load_k(1)
         load_q(range(1, 2))
-        load_v(range(1))
-        load_v(range(1, 2))
+        load_v(range(0, 1))
         load_k(2)
         load_q(range(2, 3))
-        load_v(range(2, B))
+        load_v(range(1, 2))
+        load_v(range(2, 4))
         load_k(3)
         load_q(range(3, 4))
 
@@ -347,10 +348,10 @@ def tile_radixattention_s_kernel(tc, q, k, v, k_cache, v_cache, out):
             by_pair(s - 2, quantise_e)
             when(sequence_that_starts_at(s - 4), invert_sums)
             by_pair(s - 5, normalise_and_store)
-            when(unit(s + 1), bias_of_exp)
-            when(sequence_that_starts_at(s - 3), quantise_v)
             if s >= 0:
                 when(sequence_that_starts_at(s + 4), lambda b: copy_k(b, 0, nc.vector.tensor_copy))
+            when(unit(s + 1), bias_of_exp)
+            when(sequence_that_starts_at(s - 3), quantise_v)
 
             when(unit(s), exponentials)
             when(unit(s - 1), regroup_e)

@@ -317,10 +317,10 @@ def tile_radixattention_s_kernel(tc, q, k, v, k_cache, v_cache, out):
         load_v(range(0, 1))
         load_k(2)
         load_q(range(2, 3))
-        load_v(range(1, 2))
-        load_v(range(2, 4))
         load_k(3)
         load_q(range(3, 4))
+        load_v(range(1, 2))
+        load_v(range(2, 4))
 
         for b in range(B):
             regroup_v(b, 0)

@@ -152,31 +152,30 @@ def tile_radixattention_s_kernel(tc, q, k, v, k_cache, v_cache, out):
             kT[b, g] = keep.tile([P, S], BF16, name="kT%d_%d" % (b, g))
             copy(out=kT[b, g][:], in_=kT_ps[b, g][:])
 
-        def regroup_v(b, part):
-            if part == 0:
-                v_grouped[b] = keep.tile(
-                    [P, HK * D, 4], BF16, name="v_grouped%d" % b, align_bytes=64
-                )
+        def regroup_v(b, g):
+            tag = "v_first%d" % g if b == 0 else "grouped%d" % (HK * (b - 1) + g)
+            v_grouped[b, g] = keep.tile(
+                [P, D, 4], BF16, name="v_grouped%d_%d" % (b, g), tag=tag, bufs=1, align_bytes=64
+            )
             rows = v_rows[b].rearrange("p (t c) -> p c t", t=4)
-            width = HK * D // 4
-            for i in range(2 * part, 2 * part + 2):
-                cols = slice(i * width, (i + 1) * width)
-                nc.gpsimd.tensor_scalar(
-                    out=v_grouped[b][:, cols, :],
-                    in0=rows[:, cols, :],
-                    scalar1=1.0,
-                    scalar2=0.0,
-                    op0=ALU.mult,
-                    op1=ALU.add,
-                )
+            nc.gpsimd.tensor_scalar(
+                out=v_grouped[b, g][:],
+                in0=rows[:, g * D : (g + 1) * D, :],
+                scalar1=1.0,
+                scalar2=0.0,
+                op0=ALU.mult,
+                op1=ALU.add,
+            )
 
-        def quantise_v(b):
-            v_codes[b] = keep.tile([P, HK * D], U32, name="v_codes%d" % b, align_bytes=64)
-            v_scales[b] = keep.tile([P, HK * D], U8, name="v_scales%d" % b, align_bytes=64)
+        def quantise_v(b, g):
+            if g == 0:
+                v_codes[b] = keep.tile([P, HK * D], U32, name="v_codes%d" % b, align_bytes=64)
+                v_scales[b] = keep.tile([P, HK * D], U8, name="v_scales%d" % b, align_bytes=64)
+            cols = slice(g * D, (g + 1) * D)
             nc.vector.quantize_mx(
-                out=v_codes[b][:].bitcast(FP8X4),
-                scales=v_scales[b][:],
-                in_=v_grouped[b][:].rearrange("p c t -> p (c t)"),
+                out=v_codes[b][:, cols].bitcast(FP8X4),
+                scales=v_scales[b][:, cols],
+                in_=v_grouped[b, g][:].rearrange("p c t -> p (c t)"),
             )
 
         def score(n):
@@ -241,7 +240,12 @@ def tile_radixattention_s_kernel(tc, q, k, v, k_cache, v_cache, out):
             p, a = divmod(n, G)
             if a == 0:
                 e_grouped[p] = keep.tile(
-                    [P, G, E * 4], BF16, name="e_grouped%d" % p, align_bytes=64
+                    [P, G, E * 4],
+                    BF16,
+                    name="e_grouped%d" % p,
+                    tag="grouped%d" % p,
+                    bufs=1,
+                    align_bytes=64,
                 )
             nc.scalar.copy(
                 out=e_grouped[p][:, a, :].bitcast(F32).rearrange("p (i u) -> p i u", u=2),
@@ -317,14 +321,13 @@ def tile_radixattention_s_kernel(tc, q, k, v, k_cache, v_cache, out):
         load_v(range(0, 1))
         load_k(2)
         load_q(range(2, 3))
+        load_v(range(1, 2))
         load_k(3)
         load_q(range(3, 4))
-        load_v(range(1, 2))
         load_v(range(2, 4))
 
-        for b in range(B):
-            regroup_v(b, 0)
-            regroup_v(b, 1)
+        for g in range(HK):
+            regroup_v(0, g)
 
         transpose_k(0, 0)
         copy_k(0, 0, nc.vector.tensor_copy)
@@ -345,13 +348,20 @@ def tile_radixattention_s_kernel(tc, q, k, v, k_cache, v_cache, out):
             when(sequence_that_starts_at(s + 2 if s < 0 else s + 3), lambda b: transpose_k(b, 1))
 
             when(unit(s + 1), max_scores)
+            if s == 3:
+                quantise_v(0, 0)
+                quantise_v(0, 1)
+            p = pair_that_ends_at(s - 2)
+            if p is not None and 1 <= p <= HK * (B - 1):
+                quantise_v(1 + (p - 1) // HK, (p - 1) % HK)
             by_pair(s - 2, quantise_e)
+            if p is not None and p < HK * (B - 1):
+                regroup_v(1 + p // HK, p % HK)
             when(sequence_that_starts_at(s - 4), invert_sums)
             by_pair(s - 5, normalise_and_store)
             if s >= 0:
                 when(sequence_that_starts_at(s + 4), lambda b: copy_k(b, 0, nc.vector.tensor_copy))
             when(unit(s + 1), bias_of_exp)
-            when(sequence_that_starts_at(s - 3), quantise_v)
 
             when(unit(s), exponentials)
             when(unit(s - 1), regroup_e)

@@ -343,9 +343,9 @@ def tile_radixattention_s_kernel(tc, q, k, v, k_cache, v_cache, out):
                 keep_warm(1)
             when(unit(s - 1), transpose_e)
             by_pair(s - 3, multiply_v)
+            when(sequence_that_starts_at(s + 2 if s < 0 else s + 3), lambda b: transpose_k(b, 1))
             when(sequence_that_starts_at(s + 5), lambda b: transpose_q(b, range(H)))
             when(sequence_that_starts_at(s + 5), lambda b: transpose_k(b, 0))
-            when(sequence_that_starts_at(s + 2 if s < 0 else s + 3), lambda b: transpose_k(b, 1))
 
             when(unit(s + 1), max_scores)
             if s == 3:
@@ -364,7 +364,7 @@ def tile_radixattention_s_kernel(tc, q, k, v, k_cache, v_cache, out):
             when(unit(s + 1), bias_of_exp)
 
             when(unit(s), exponentials)
-            when(unit(s - 1), regroup_e)
             if s >= 0:
                 when(sequence_that_starts_at(s + 4), lambda b: copy_q(b, range(H)))
             when(sequence_that_starts_at(s + 1 if s < 0 else s + 2), lambda b: copy_k(b, 1, nc.scalar.copy))
+            when(unit(s - 1), regroup_e)

@@ -203,24 +203,36 @@ def tile_radixattention_s_kernel(tc, q, k, v, k_cache, v_cache, out):
 
         def max_scores(n):
             b, h = divmod(n, H)
-            nc.vector.tensor_reduce(
-                out=row_max[b][:, h : h + 1], in_=score_ps[n][:], axis=AXIS.X, op=ALU.max
-            )
+            e_rows[n] = keep.tile([P, S], BF16, name="e_rows%d" % n)
+            if b == 0:
+                nc.vector.tensor_scalar(
+                    out=e_rows[n][:],
+                    in0=score_ps[n][:],
+                    scalar1=-SCALING,
+                    scalar2=None,
+                    op0=ALU.mult,
+                    op1=ALU.min,
+                    accum_out=exp_bias[b][:, h : h + 1],
+                )
+            else:
+                nc.vector.tensor_reduce(
+                    out=row_max[b][:, h : h + 1], in_=score_ps[n][:], axis=AXIS.X, op=ALU.max
+                )
 
         def bias_of_exp(n):
             b, h = divmod(n, H)
-            nc.vector.tensor_scalar(
-                out=exp_bias[b][:, h : h + 1],
-                in0=row_max[b][:, h : h + 1],
-                scalar1=-SCALING,
-                scalar2=SHIFT,
-                op0=ALU.mult,
-                op1=ALU.add,
-            )
+            if b > 0:
+                nc.vector.tensor_scalar(
+                    out=exp_bias[b][:, h : h + 1],
+                    in0=row_max[b][:, h : h + 1],
+                    scalar1=-SCALING,
+                    scalar2=SHIFT,
+                    op0=ALU.mult,
+                    op1=ALU.add,
+                )
 
         def exponentials(n):
             b, h = divmod(n, H)
-            e_rows[n] = keep.tile([P, S], BF16, name="e_rows%d" % n)
             nc.scalar.activation(
                 out=e_rows[n][:].rearrange("p (u j x) -> p u j x", u=2, x=2),
                 in_=score_ps[n][:].rearrange("p (j u x) -> p u j x", u=2, x=2),
@@ -236,7 +248,7 @@ def tile_radixattention_s_kernel(tc, q, k, v, k_cache, v_cache, out):
             for u in range(2):
                 nc.tensor.transpose(eT_ps[n][:, u, :], words[:, u * P : (u + 1) * P], ident_f32[:])
 
-        def regroup_e(n):
+        def regroup_e(n, copy):
             p, a = divmod(n, G)
             if a == 0:
                 e_grouped[p] = keep.tile(
@@ -247,7 +259,7 @@ def tile_radixattention_s_kernel(tc, q, k, v, k_cache, v_cache, out):
                     bufs=1,
                     align_bytes=64,
                 )
-            nc.scalar.copy(
+            copy(
                 out=e_grouped[p][:, a, :].bitcast(F32).rearrange("p (i u) -> p i u", u=2),
                 in_=eT_ps[n][:].rearrange("p u i -> p i u"),
             )
@@ -338,10 +350,13 @@ def tile_radixattention_s_kernel(tc, q, k, v, k_cache, v_cache, out):
         keep_warm(1)
 
         for s in range(-2, N_HEADS + 5):
+            if s < 2:
+                when(unit(s - 1), transpose_e)
             when(unit(s + 2), score)
             if s == -2:
                 keep_warm(1)
-            when(unit(s - 1), transpose_e)
+            if s >= 2:
+                when(unit(s - 1), transpose_e)
             by_pair(s - 3, multiply_v)
             when(sequence_that_starts_at(s + 2 if s < 0 else s + 3), lambda b: transpose_k(b, 1))
             when(sequence_that_starts_at(s + 5), lambda b: transpose_q(b, range(H)))
@@ -357,14 +372,21 @@ def tile_radixattention_s_kernel(tc, q, k, v, k_cache, v_cache, out):
             by_pair(s - 2, quantise_e)
             if p is not None and p < HK * (B - 1):
                 regroup_v(1 + p // HK, p % HK)
-            when(sequence_that_starts_at(s - 4), invert_sums)
+            if s == N_HEADS - 2:
+                invert_sums(B - 2)
+                bias_of_exp(s + 1)
+                regroup_e(s - 1, nc.vector.tensor_copy)
+            elif s != H * (B - 2) + 4:
+                when(sequence_that_starts_at(s - 4), invert_sums)
             by_pair(s - 5, normalise_and_store)
             if s >= 0:
                 when(sequence_that_starts_at(s + 4), lambda b: copy_k(b, 0, nc.vector.tensor_copy))
-            when(unit(s + 1), bias_of_exp)
+            if s != N_HEADS - 2:
+                when(unit(s + 1), bias_of_exp)
 
             when(unit(s), exponentials)
             if s >= 0:
                 when(sequence_that_starts_at(s + 4), lambda b: copy_q(b, range(H)))
             when(sequence_that_starts_at(s + 1 if s < 0 else s + 2), lambda b: copy_k(b, 1, nc.scalar.copy))
-            when(unit(s - 1), regroup_e)
+            if s != N_HEADS - 2:
+                when(unit(s - 1), lambda n: regroup_e(n, nc.scalar.copy))

import math
from contextlib import ExitStack

import concourse.mybir as mybir
from concourse.masks import make_identity

BF16 = mybir.dt.bfloat16
F32 = mybir.dt.float32
U32 = mybir.dt.uint32
U8 = mybir.dt.uint8
FP8X4 = mybir.dt.float8_e4m3fn_x4
ALU = mybir.AluOpType
ACT = mybir.ActivationFunctionType
AXIS = mybir.AxisListType

B = 4
E = 128
PREFIX = 384
S = PREFIX + E
H = 4
HK = 2
G = H // HK
D = 128
P = 128
SCALING = 1.0 / math.sqrt(D)
SHIFT = 3 * math.log(2.0)
HIDDEN = -1.0e30

FLOPS = 2 * 2 * B * H * E * S * D


N_HEADS = B * H
N_PAIRS = B * HK


def sequence_that_starts_at(n):
    return n // H if 0 <= n < N_HEADS and n % H == 0 else None


def pair_that_ends_at(n):
    return n // G if 0 <= n < N_HEADS and n % G == G - 1 else None


def tile_radixattention_s_kernel(tc, q, k, v, k_cache, v_cache, out):
    nc = tc.nc
    with ExitStack() as ctx:
        consts = ctx.enter_context(tc.tile_pool(name="consts", bufs=1))
        keep = ctx.enter_context(tc.tile_pool(name="keep", bufs=1))
        banks = ctx.enter_context(tc.psum_pool(name="banks", bufs=1))
        ctx.enter_context(tc.manual_schedule())

        ident_bf = consts.tile([P, P], BF16, name="ident_bf")
        make_identity(nc, ident_bf[:])
        hidden_t = consts.tile([P, E], F32, name="hidden_t")
        nc.gpsimd.memset(hidden_t[:], 0.0)
        nc.gpsimd.affine_select(
            out=hidden_t[:],
            in_=hidden_t[:],
            compare_op=ALU.is_ge,
            fill=HIDDEN,
            base=0,
            pattern=[[1, E]],
            channel_multiplier=-1,
        )
        ident_f32 = consts.tile([P, P], F32, name="ident_f32")
        make_identity(nc, ident_f32[:])
        warm_in = consts.tile([P, 1], F32, name="warm_in")
        warm_out = consts.tile([P, 1], F32, name="warm_out")
        nc.vector.memset(warm_in[:], 0.0)
        nc.scalar.activation(out=warm_out[:], in_=warm_in[:], func=ACT.Exp)

        zeros = consts.tile([P, P], F32, name="zeros")
        nc.vector.memset(zeros[:], 0.0)

        def keep_warm(count):
            for i in range(count):
                warm_ps = banks.tile([P, P], F32, name="warm_ps", tag="o", bufs=2)
                nc.tensor.matmul(out=warm_ps[:], lhsT=zeros[:], rhs=zeros[:], start=True, stop=True)

        keep_warm(4)

        q_rows, k_rows, v_rows = {}, {}, {}
        qT_ps, kT_ps, qT, kT = {}, {}, {}, {}
        v_grouped, v_codes, v_scales = {}, {}, {}
        row_max, exp_bias, row_sum, inv_sum = {}, {}, {}, {}
        score_ps, e_rows = {}, {}
        eT_ps, e_grouped, e_codes, e_scales, o_ps = {}, {}, {}, {}, {}

        def load_k(b, heads=range(HK)):
            if heads.start == 0:
                k_rows[b] = keep.tile([P, S // P, HK * D], BF16, name="k_rows%d" % b)
            cols = slice(heads.start * D, heads.stop * D)
            span = slice(heads.start, heads.stop)
            nc.sync.dma_start(
                out=k_rows[b][:, 0 : PREFIX // P, cols],
                in_=k_cache[b, :, span].rearrange("(t p) g d -> p t (g d)", p=P),
            )
            nc.sync.dma_start(
                out=k_rows[b][:, PREFIX // P, cols], in_=k[b, :, span].rearrange("e g d -> e (g d)")
            )

        def load_q(sequences):
            rows = keep.tile([P, len(sequences), H * D], BF16, name="q_rows%d" % sequences.start)
            nc.sync.dma_start(
                out=rows[:],
                in_=q[sequences.start : sequences.stop].rearrange("b e h d -> e b (h d)"),
            )
            for i, b in enumerate(sequences):
                q_rows[b] = rows[:, i, :]

        def load_v(sequences):
            rows = keep.tile(
                [P, len(sequences), 4 * HK * D], BF16, name="v_rows%d" % sequences.start
            )
            span = slice(sequences.start, sequences.stop)
            for partitions, source in (
                (slice(0, 64), v_cache[span, 0:256]),
                (slice(64, 96), v_cache[span, 256:PREFIX]),
                (slice(96, P), v[span]),
            ):
                nc.sync.dma_start(
                    out=rows[partitions],
                    in_=source.rearrange("b (p t) g d -> p b (t g d)", t=4),
                )
            for i, b in enumerate(sequences):
                v_rows[b] = rows[:, i, :]

        def transpose_q(b, heads):
            qT_ps[b, heads.start] = banks.tile([P, H * E], BF16, name="qT_ps", tag="work", bufs=3)
            for h in heads:
                cols = slice(h * D, (h + 1) * D)
                nc.tensor.transpose(
                    qT_ps[b, heads.start][:, cols], q_rows[b][:, cols], ident_bf[:]
                )

        def transpose_k(b, g):
            kT_ps[b, g] = banks.tile([P, S], BF16, name="kT_ps", tag="work", bufs=3)
            for t in range(S // P):
                nc.tensor.transpose(
                    kT_ps[b, g][:, t * P : (t + 1) * P],
                    k_rows[b][:, t, g * D : (g + 1) * D],
                    ident_bf[:],
                )

        def copy_q(b, heads):
            if heads.start == 0:
                qT[b] = keep.tile([P, H * E], BF16, name="qT%d" % b)
            cols = slice(heads.start * E, heads.stop * E)
            nc.scalar.copy(out=qT[b][:, cols], in_=qT_ps[b, heads.start][:, cols])

        def copy_k(b, g, copy):
            kT[b, g] = keep.tile([P, S], BF16, name="kT%d_%d" % (b, g))
            copy(out=kT[b, g][:], in_=kT_ps[b, g][:])

        def regroup_v(b, g):
            tag = "v_first%d" % g if b == 0 else "grouped%d" % (HK * (b - 1) + g)
            v_grouped[b, g] = keep.tile(
                [P, D, 4], BF16, name="v_grouped%d_%d" % (b, g), tag=tag, bufs=1, align_bytes=64
            )
            rows = v_rows[b].rearrange("p (t c) -> p c t", t=4)
            nc.gpsimd.tensor_scalar(
                out=v_grouped[b, g][:],
                in0=rows[:, g * D : (g + 1) * D, :],
                scalar1=1.0,
                scalar2=0.0,
                op0=ALU.mult,
                op1=ALU.add,
            )

        def quantise_v(b, g):
            if g == 0:
                v_codes[b] = keep.tile([P, HK * D], U32, name="v_codes%d" % b, align_bytes=64)
                v_scales[b] = keep.tile([P, HK * D], U8, name="v_scales%d" % b, align_bytes=64)
            cols = slice(g * D, (g + 1) * D)
            nc.vector.quantize_mx(
                out=v_codes[b][:, cols].bitcast(FP8X4),
                scales=v_scales[b][:, cols],
                in_=v_grouped[b, g][:].rearrange("p c t -> p (c t)"),
            )

        def score(n):
            b, h = divmod(n, H)
            if h == 0:
                row_max[b] = keep.tile([P, H], F32, name="row_max%d" % b)
                exp_bias[b] = keep.tile([P, H], F32, name="exp_bias%d" % b)
                row_sum[b] = keep.tile([P, H], F32, name="row_sum%d" % b)
            score_ps[n] = banks.tile([P, S], F32, name="score_ps", tag="score", bufs=3)
            nc.tensor.matmul(
                out=score_ps[n][:],
                lhsT=qT[b][:, h * E : (h + 1) * E],
                rhs=kT[b, h // G][:],
                start=True,
                stop=False,
            )
            nc.tensor.matmul(
                out=score_ps[n][:, PREFIX:S],
                lhsT=hidden_t[:],
                rhs=ident_f32[:],
                is_transpose=True,
                start=False,
                stop=True,
            )

        def max_scores(n):
            b, h = divmod(n, H)
            e_rows[n] = keep.tile([P, S], BF16, name="e_rows%d" % n)
            if b == 0:
                nc.vector.tensor_scalar(
                    out=e_rows[n][:],
                    in0=score_ps[n][:],
                    scalar1=-SCALING,
                    scalar2=None,
                    op0=ALU.mult,
                    op1=ALU.min,
                    accum_out=exp_bias[b][:, h : h + 1],
                )
            else:
                nc.vector.tensor_reduce(
                    out=row_max[b][:, h : h + 1], in_=score_ps[n][:], axis=AXIS.X, op=ALU.max
                )

        def bias_of_exp(n):
            b, h = divmod(n, H)
            if b > 0:
                nc.vector.tensor_scalar(
                    out=exp_bias[b][:, h : h + 1],
                    in0=row_max[b][:, h : h + 1],
                    scalar1=-SCALING,
                    scalar2=SHIFT,
                    op0=ALU.mult,
                    op1=ALU.add,
                )

        def exponentials(n):
            b, h = divmod(n, H)
            nc.scalar.activation(
                out=e_rows[n][:].rearrange("p (u j x) -> p u j x", u=2, x=2),
                in_=score_ps[n][:].rearrange("p (j u x) -> p u j x", u=2, x=2),
                func=ACT.Exp,
                bias=exp_bias[b][:, h : h + 1],
                scale=SCALING,
                accum_out=row_sum[b][:, h : h + 1],
            )

        def transpose_e(n):
            eT_ps[n] = banks.tile([P, 2, E], F32, name="eT_ps", tag="work", bufs=3)
            words = e_rows[n][:].bitcast(F32)
            for u in range(2):
                nc.tensor.transpose(eT_ps[n][:, u, :], words[:, u * P : (u + 1) * P], ident_f32[:])

        def regroup_e(n, copy):
            p, a = divmod(n, G)
            if a == 0:
                e_grouped[p] = keep.tile(
                    [P, G, E * 4],
                    BF16,
                    name="e_grouped%d" % p,
                    tag="grouped%d" % p,
                    bufs=1,
                    align_bytes=64,
                )
            copy(
                out=e_grouped[p][:, a, :].bitcast(F32).rearrange("p (i u) -> p i u", u=2),
                in_=eT_ps[n][:].rearrange("p u i -> p i u"),
            )

        def quantise_e(p, heads):
            if heads.start == 0:
                e_codes[p] = keep.tile([P, G * E], U32, name="e_codes%d" % p, align_bytes=64)
                e_scales[p] = keep.tile([P, G * E], U8, name="e_scales%d" % p, align_bytes=64)
            cols = slice(heads.start * E, heads.stop * E)
            nc.vector.quantize_mx(
                out=e_codes[p][:, cols].bitcast(FP8X4),
                scales=e_scales[p][:, cols],
                in_=e_grouped[p][:, heads.start : heads.stop, :].rearrange("p a c -> p (a c)"),
            )

        def multiply_v(p, heads):
            b, g = divmod(p, HK)
            tag, bufs = ("o", 2) if len(heads) == G else ("score", 3)
            o_ps[p, heads.start] = banks.tile([P, G, HK * D], F32, name="o_ps", tag=tag, bufs=bufs)
            v_cols = slice(0, HK * D) if len(heads) == G else slice(g * D, (g + 1) * D)
            for a in heads:
                nc.tensor.matmul_mx(
                    out=o_ps[p, heads.start][:, a, v_cols],
                    lhsT=e_codes[p][:, a * E : (a + 1) * E].bitcast(FP8X4),
                    lhsT_scale=e_scales[p][:, a * E : (a + 1) * E],
                    rhs=v_codes[b][:, v_cols].bitcast(FP8X4),
                    rhs_scale=v_scales[b][:, v_cols],
                    start=True,
                    stop=True,
                )

        def invert_sums(b):
            inv_sum[b] = keep.tile([P, H], F32, name="inv_sum%d" % b)
            nc.vector.reciprocal(out=inv_sum[b][:], in_=row_sum[b][:])

        def normalise_and_store(p, heads):
            b, g = divmod(p, HK)
            count = len(heads)
            first = g * G + heads.start
            o_sb = keep.tile([P, count, D], F32, name="o_sb%d_%d" % (p, heads.start))
            nc.vector.tensor_tensor(
                out=o_sb[:],
                in0=o_ps[p, heads.start][:, heads.start : heads.stop, g * D : (g + 1) * D],
                in1=inv_sum[b][:, first : first + count].unsqueeze(2).to_broadcast([P, count, D]),
                op=ALU.mult,
            )
            nc.sync.dma_start(
                out=out[b * E : (b + 1) * E, first * D : (first + count) * D],
                in_=o_sb[:].rearrange("p a d -> p (a d)"),
            )

        def when(index, stage):
            if index is not None:
                stage(index)

        def unit(n):
            return n if 0 <= n < N_HEADS else None

        def by_pair(n, stage):
            p, a = divmod(n, G)
            if p == N_PAIRS - 1:
                stage(p, range(a, a + 1))
            elif 0 <= p < N_PAIRS and a == G - 1:
                stage(p, range(G))

        load_k(0, range(1))
        load_q(range(1))
        load_k(0, range(1, HK))
        load_k(1)
        load_q(range(1, 2))
        load_v(range(0, 1))
        load_k(2)
        load_q(range(2, 3))
        load_v(range(1, 2))
        load_k(3)
        load_q(range(3, 4))
        load_v(range(2, 4))

        for g in range(HK):
            regroup_v(0, g)

        transpose_k(0, 0)
        copy_k(0, 0, nc.vector.tensor_copy)
        transpose_q(0, range(1))
        copy_q(0, range(1))
        transpose_q(0, range(1, H))
        copy_q(0, range(1, H))
        keep_warm(1)

        for s in range(-2, N_HEADS + 5):
            if s < 2:
                when(unit(s - 1), transpose_e)
            when(unit(s + 2), score)
            if s == -2:
                keep_warm(1)
            if s >= 2:
                when(unit(s - 1), transpose_e)
            by_pair(s - 3, multiply_v)
            when(sequence_that_starts_at(s + 2 if s < 0 else s + 3), lambda b: transpose_k(b, 1))
            when(sequence_that_starts_at(s + 5), lambda b: transpose_q(b, range(H)))
            when(sequence_that_starts_at(s + 5), lambda b: transpose_k(b, 0))

            when(unit(s + 1), max_scores)
            if s == 3:
                quantise_v(0, 0)
                quantise_v(0, 1)
            p = pair_that_ends_at(s - 2)
            if p is not None and 1 <= p <= HK * (B - 1):
                quantise_v(1 + (p - 1) // HK, (p - 1) % HK)
            by_pair(s - 2, quantise_e)
            if p is not None and p < HK * (B - 1):
                regroup_v(1 + p // HK, p % HK)
            if s == N_HEADS - 2:
                invert_sums(B - 2)
                bias_of_exp(s + 1)
                regroup_e(s - 1, nc.vector.tensor_copy)
            elif s != H * (B - 2) + 4:
                when(sequence_that_starts_at(s - 4), invert_sums)
            by_pair(s - 5, normalise_and_store)
            if s >= 0:
                when(sequence_that_starts_at(s + 4), lambda b: copy_k(b, 0, nc.vector.tensor_copy))
            if s != N_HEADS - 2:
                when(unit(s + 1), bias_of_exp)

            when(unit(s), exponentials)
            if s >= 0:
                when(sequence_that_starts_at(s + 4), lambda b: copy_q(b, range(H)))
            when(sequence_that_starts_at(s + 1 if s < 0 else s + 2), lambda b: copy_k(b, 1, nc.scalar.copy))
            if s != N_HEADS - 2:
                when(unit(s - 1), lambda n: regroup_e(n, nc.scalar.copy))
